import numpy as np
import ml_dtypes


def mxq(x, axis, fmt="e4m3"):
    dtype, down = {"e4m3": (ml_dtypes.float8_e4m3fn, 7), "e5m2": (ml_dtypes.float8_e5m2, 14)}[fmt]
    v = np.moveaxis(np.asarray(x, np.float32).astype(ml_dtypes.bfloat16).astype(np.float64), axis, -1)
    blocks = v.reshape(v.shape[:-1] + (-1, 32))
    amax = np.abs(blocks).max(-1, keepdims=True)
    byte = np.maximum(np.where(amax > 0, np.frexp(amax)[1] - 1 + 127, 0) - down, 1)
    scale = np.exp2(byte - 127.0)
    codes = (blocks / scale).astype(np.float32).astype(dtype).astype(np.float64)
    return np.moveaxis((codes * scale).reshape(v.shape), -1, axis)


WIDE = False


def mx_kscale(k):
    if not WIDE:
        return np.ones(k)
    levels = np.array([10, -10, 5, -5, 0])
    a = np.random.permutation(np.resize(levels, k // 512 * 4)).reshape(k // 512, 4)
    idx = np.arange(k)
    return np.exp2(a[idx // 512, idx % 128 // 32])


BF16 = ml_dtypes.bfloat16


def bf(x):
    return np.asarray(x, np.float32).astype(BF16)


def f64(x):
    return np.asarray(x).astype(np.float64)


B, N, HID, ITERS = 512, 32, 2048, 10
DOUT = N * N
SLOPE = 0.01
EPS = 1e-8


def leaky(v):
    return np.where(v >= 0.0, v, SLOPE * v)


def l1_normalize(r, axis):
    return r / np.maximum(np.abs(r).sum(axis=axis, keepdims=True), EPS)


def setup_inputs():
    s, t = mx_kscale(HID), mx_kscale(HID)
    return {"h3": bf(leaky(np.random.standard_normal((B, HID)) * 1.1) * s),
            "W4": bf(np.random.standard_normal((HID, HID)) * 1.4 / np.sqrt(HID) / s[:, None] * t),
            "b4": bf(np.random.standard_normal(HID) * 0.3 * t),
            "W5": bf(np.random.standard_normal((HID, DOUT)) * 2.0 / np.sqrt(HID) / t[:, None]),
            "b5": bf(np.random.standard_normal(DOUT) * 3.0 - 4.0)}


def reference(h3, W4, b4, W5, b5):
    h4 = leaky((mxq(f64(h3), 1, "e4m3") @ mxq(f64(W4), 0, "e4m3")) + f64(b4))
    r = ((mxq(h4, 1, "e4m3") @ mxq(f64(W5), 0, "e4m3")) + f64(b5)).reshape(B, N, N)
    r = np.logaddexp(r, 0.0)
    for _ in range(ITERS):
        r = l1_normalize(r, 1)
        r = l1_normalize(r, 2)
    return r

@@ -1,0 +1,312 @@
+from contextlib import ExitStack
+
+import concourse.mybir as mybir
+from concourse.masks import make_identity
+
+F32 = mybir.dt.float32
+BF16 = mybir.dt.bfloat16
+U32 = mybir.dt.uint32
+U8 = mybir.dt.uint8
+FP8X4 = mybir.dt.float8_e4m3fn_x4
+ALU = mybir.AluOpType
+ACT = mybir.ActivationFunctionType
+AXIS = mybir.AxisListType
+
+P = 128
+PACK = 4
+K_PASS = P * PACK
+BATCH, SIDE, HID, ROUNDS = 512, 32, 2048, 10
+DOUT = SIDE * SIDE
+SLOPE = 0.01
+EPS = 1e-8
+PASSES = HID // K_PASS
+BATCH_TILES = BATCH // P
+BANK = 512
+W_CHUNK = 1024
+RUN = 4
+VECTOR_COLS = 512
+I_LO = P // SIDE
+LINEAR_FROM = 30.0
+VECTOR_TILES = 2
+
+FLOPS = 2 * BATCH * HID * (HID + DOUT)
+
+
+def regroup(nc, stage, raw):
+    grouped = stage.tile([P, W_CHUNK, PACK], BF16, align_bytes=64, name="grouped")
+    src = raw[:].rearrange("p t (c i) -> p c t i", i=RUN)
+    dst = grouped[:].rearrange("p (c i) t -> p c t i", i=RUN)
+    cut = VECTOR_COLS // RUN
+    nc.vector.tensor_copy(out=dst[:, :cut], in_=src[:, :cut])
+    nc.scalar.copy(out=dst[:, cut:], in_=src[:, cut:])
+    return grouped
+
+
+def quantise(nc, grouped, codes, scales):
+    nc.vector.quantize_mx(out=codes.bitcast(FP8X4), scales=scales, in_=grouped)
+
+
+def tile_matchingnet_pa_kernel(tc, h3, W4, b4, W5, b5, out):
+    nc = tc.nc
+    with ExitStack() as whole:
+        consts = whole.enter_context(tc.tile_pool(name="consts", bufs=1))
+        banks = whole.enter_context(tc.psum_pool(name="banks", bufs=8))
+
+        ident = consts.tile([P, P], F32, name="ident")
+        make_identity(nc, ident[:])
+        swap = consts.tile([P, P], F32, name="swap")
+        nc.vector.tensor_copy(
+            out=swap[:].rearrange("p (j i) -> p j i", i=I_LO),
+            in_=ident[:].rearrange("p (i j) -> p j i", i=I_LO),
+        )
+
+        b4_rows = HID // P
+        b5_rows = DOUT // P
+        bias_rows = consts.tile([P, P], BF16, name="bias_rows")
+        nc.vector.memset(bias_rows[:], 0.0)
+        nc.scalar.dma_start(out=bias_rows[0:b4_rows, :], in_=b4.rearrange("(r c) -> r c", c=P))
+        nc.scalar.dma_start(
+            out=bias_rows[b4_rows : b4_rows + b5_rows, :], in_=b5.rearrange("(r c) -> r c", c=P)
+        )
+        bias_rows_f32 = consts.tile([P, P], F32, name="bias_rows_f32")
+        nc.vector.tensor_copy(out=bias_rows_f32[:], in_=bias_rows[:])
+        bias_bank = banks.tile([P, P], F32, tag="bank", name="bias_bank")
+        nc.tensor.transpose(bias_bank[:], bias_rows_f32[:], ident[:])
+        bias_cols = consts.tile([P, b4_rows + b5_rows], F32, name="bias_cols")
+        nc.vector.tensor_copy(out=bias_cols[:], in_=bias_bank[:, 0 : b4_rows + b5_rows])
+
+        z_banks = []
+        with ExitStack() as front:
+            keep = front.enter_context(tc.tile_pool(name="keep", bufs=1))
+            wraw = front.enter_context(tc.tile_pool(name="wraw", bufs=4))
+            stage = front.enter_context(tc.tile_pool(name="stage", bufs=3))
+            acts = front.enter_context(tc.tile_pool(name="acts", bufs=2))
+
+            h3_rows = []
+            for bt in range(BATCH_TILES):
+                rows = keep.tile([P, HID], BF16, name="h3_rows%d" % bt)
+                nc.sync.dma_start(out=rows[:], in_=h3[bt * P : (bt + 1) * P, :])
+                h3_rows.append(rows)
+            h3_grouped = [
+                keep.tile([P, BATCH * PACK], BF16, align_bytes=64, name="h3_grouped%d" % g)
+                for g in range(PASSES)
+            ]
+            h3_codes = keep.tile([P, PASSES, BATCH], U32, align_bytes=64, name="h3_codes")
+            h3_scales = keep.tile([P, PASSES, BATCH], U8, align_bytes=64, name="h3_scales")
+            for pair in range(BATCH_TILES // 2):
+                for g in range(PASSES):
+                    flipped = banks.tile([P, 2, 2, P], F32, tag="bank", name="flipped")
+                    for c in range(2):
+                        words = h3_rows[2 * pair + c][:].bitcast(F32)
+                        for u in range(2):
+                            first = (K_PASS // 2) * g + P * u
+                            nc.tensor.transpose(flipped[:, c, u, :], words[:, first : first + P], ident[:])
+                    dst = (
+                        h3_grouped[g][:]
+                        .bitcast(F32)
+                        .rearrange("p (b u) -> p b u", u=2)[:, 2 * P * pair : 2 * P * (pair + 1), :]
+                        .rearrange("p (c b) u -> p c b u", c=2)
+                    )
+                    src = flipped[:].rearrange("p c u b -> p c b u")
+                    if g % 2 == 0:
+                        nc.vector.tensor_copy(out=dst, in_=src)
+                    else:
+                        nc.scalar.copy(out=dst, in_=src)
+            for g in range(PASSES):
+                quantise(nc, h3_grouped[g][:], h3_codes[:, g, :], h3_scales[:, g, :])
+
+            w4_codes = keep.tile([P, PASSES, HID], U32, align_bytes=64, name="w4_codes")
+            w4_scales = keep.tile([P, PASSES, HID], U8, align_bytes=64, name="w4_scales")
+            w5_codes = keep.tile([P, PASSES, DOUT], U32, align_bytes=64, name="w5_codes")
+            w5_scales = keep.tile([P, PASSES, DOUT], U8, align_bytes=64, name="w5_scales")
+            h4_codes = keep.tile([P, PASSES, BATCH], U32, align_bytes=64, name="h4_codes")
+            h4_scales = keep.tile([P, PASSES, BATCH], U8, align_bytes=64, name="h4_scales")
+
+            def load_w4(block, g):
+                raw = wraw.tile([P, PACK, W_CHUNK], BF16, name="raw")
+                for u in range(2):
+                    first = K_PASS * g + (K_PASS // 2) * u
+                    rows = W4[first : first + K_PASS // 2, W_CHUNK * block : W_CHUNK * (block + 1)]
+                    nc.sync.dma_start(
+                        out=raw[:, 2 * u : 2 * u + 2, :], in_=rows.rearrange("(q e) c -> q e c", e=2)
+                    )
+                return raw
+
+            def load_w5(g):
+                raw = wraw.tile([P, PACK, W_CHUNK], BF16, name="raw")
+                rows = W5[K_PASS * g : K_PASS * (g + 1), :]
+                nc.sync.dma_start(out=raw[:], in_=rows.rearrange("(t p) n -> p t n", p=P))
+                return raw
+
+            tiles_per_block = W_CHUNK // P
+            for block in range(HID // W_CHUNK):
+                h4_banks = [
+                    banks.tile([P, BANK], F32, tag="bank", name="h4_bank%d" % m) for m in range(tiles_per_block)
+                ]
+                cols = slice(W_CHUNK * block, W_CHUNK * (block + 1))
+                for g in range(PASSES):
+                    grouped = regroup(nc, stage, load_w4(block, g))
+                    quantise(
+                        nc, grouped[:].rearrange("p w t -> p (w t)"), w4_codes[:, g, cols], w4_scales[:, g, cols]
+                    )
+                    for m in range(tiles_per_block):
+                        first = W_CHUNK * block + P * m
+                        nc.tensor.matmul_mx(
+                            out=h4_banks[m][:],
+                            lhsT=w4_codes[:, g, first : first + P].bitcast(FP8X4),
+                            lhsT_scale=w4_scales[:, g, first : first + P],
+                            rhs=h3_codes[:, g, :].bitcast(FP8X4),
+                            rhs_scale=h3_scales[:, g, :],
+                            start=(g == 0),
+                            stop=(g == PASSES - 1),
+                        )
+                for quad in range(tiles_per_block // PACK):
+                    g2 = (tiles_per_block // PACK) * block + quad
+                    biased = acts.tile([P, PACK, BATCH], F32, name="biased")
+                    for t in range(PACK):
+                        m = PACK * g2 + t
+                        nc.scalar.activation(
+                            out=biased[:, t, :],
+                            in_=h4_banks[PACK * quad + t][:],
+                            func=ACT.Identity,
+                            bias=bias_cols[:, m : m + 1],
+                            scale=1.0,
+                        )
+                    h4_grouped = acts.tile([P, BATCH, PACK], BF16, align_bytes=64, name="h4_grouped")
+                    by_column = biased[:].rearrange("p t b -> p b t")
+                    nc.vector.scalar_tensor_tensor(
+                        out=h4_grouped[:], in0=by_column, scalar=SLOPE, in1=by_column, op0=ALU.mult, op1=ALU.max
+                    )
+                    quantise(
+                        nc, h4_grouped[:].rearrange("p b t -> p (b t)"), h4_codes[:, g2, :], h4_scales[:, g2, :]
+                    )
+
+            z_banks = [banks.tile([P, BANK], F32, tag="bank", name="z_bank%d" % d) for d in range(DOUT // P)]
+            for g in range(PASSES):
+                grouped = regroup(nc, stage, load_w5(g))
+                quantise(nc, grouped[:].rearrange("p w t -> p (w t)"), w5_codes[:, g, :], w5_scales[:, g, :])
+                for d in range(DOUT // P):
+                    nc.tensor.matmul_mx(
+                        out=z_banks[d][:],
+                        lhsT=w5_codes[:, g, P * d : P * (d + 1)].bitcast(FP8X4),
+                        lhsT_scale=w5_scales[:, g, P * d : P * (d + 1)],
+                        rhs=h4_codes[:, g, :].bitcast(FP8X4),
+                        rhs_scale=h4_scales[:, g, :],
+                        start=(g == 0),
+                        stop=(g == PASSES - 1),
+                    )
+
+        with ExitStack() as back:
+            soft = back.enter_context(tc.tile_pool(name="soft", bufs=1))
+            work = back.enter_context(tc.tile_pool(name="work", bufs=6))
+
+            d_tiles = DOUT // P
+            expo = soft.tile([P, d_tiles, BATCH], F32, name="expo")
+            r_flipped = soft.tile([P, d_tiles, BATCH], F32, name="r_flipped")
+            for d in range(d_tiles):
+                b5_col = bias_cols[:, b4_rows + d : b4_rows + d + 1]
+                nc.vector.tensor_scalar(
+                    out=expo[:, d, :], in0=z_banks[d][:], scalar1=b5_col, scalar2=LINEAR_FROM, op0=ALU.add, op1=ALU.min
+                )
+                nc.scalar.activation(out=expo[:, d, :], in_=expo[:, d, :], func=ACT.Exp)
+            for d in range(d_tiles):
+                b5_col = bias_cols[:, b4_rows + d : b4_rows + d + 1]
+                nc.scalar.activation(out=expo[:, d, :], in_=expo[:, d, :], func=ACT.Ln, bias=1.0, scale=1.0)
+                nc.vector.scalar_tensor_tensor(
+                    out=r_flipped[:, d, :], in0=z_banks[d][:], scalar=b5_col, in1=expo[:, d, :], op0=ALU.add, op1=ALU.max
+                )
+
+            halves = DOUT // BANK
+            per_half = BANK // P
+            by_row = {}
+            by_col = {}
+            for bt in reversed(range(BATCH_TILES)):
+                for label, layout, order in (("row", by_row, ident), ("col", by_col, swap)):
+                    pieces = []
+                    for h in range(halves):
+                        bank = banks.tile([P, BANK], F32, tag="bank", name="r_bank")
+                        for q in range(per_half):
+                            nc.tensor.transpose(
+                                bank[:, P * q : P * (q + 1)],
+                                r_flipped[:, per_half * h + q, P * bt : P * (bt + 1)],
+                                order[:],
+                            )
+                        if bt < VECTOR_TILES:
+                            pieces.append(bank)
+                        else:
+                            copy = soft.tile([P, BANK], F32, name="r_%s_%d_%d" % (label, bt, h))
+                            nc.scalar.copy(out=copy[:], in_=bank[:])
+                            pieces.append(copy)
+                    layout[bt] = pieces
+
+            state = []
+            for bt in range(BATCH_TILES):
+                vectors = {}
+                for name in ("a", "c", "floor_a", "floor_c"):
+                    vectors[name] = soft.tile([P, SIDE], F32, name="%s%d" % (name, bt))
+                    nc.vector.memset(vectors[name][:], 1.0)
+                vectors["sums"] = soft.tile([P, SIDE], F32, name="sums%d" % bt)
+                state.append(vectors)
+
+            def renew(vectors, floor, factor):
+                nc.vector.scalar_tensor_tensor(
+                    out=vectors[floor][:],
+                    in0=vectors[floor][:],
+                    scalar=EPS,
+                    in1=vectors["sums"][:],
+                    op0=ALU.mult,
+                    op1=ALU.max,
+                )
+                nc.vector.reciprocal(out=vectors[factor][:], in_=vectors[floor][:])
+
+            i_hi_half = SIDE // I_LO // halves
+            i_half = SIDE // halves
+            for rnd in range(ROUNDS):
+                for bt in range(BATCH_TILES):
+                    engine = nc.vector if bt < VECTOR_TILES else nc.gpsimd
+                    vectors = state[bt]
+                    prod = work.tile([P, DOUT], F32, name="prod")
+                    for h in range(halves):
+                        a_part = vectors["a"][:, i_half * h : i_half * (h + 1)].rearrange("p (d i) -> p d i", i=I_LO)
+                        engine.tensor_tensor(
+                            out=prod[:, BANK * h : BANK * (h + 1)].rearrange("p (d j i) -> p d j i", j=SIDE, i=I_LO),
+                            in0=by_col[bt][h][:].rearrange("p (d j i) -> p d j i", j=SIDE, i=I_LO),
+                            in1=a_part.unsqueeze(2).to_broadcast([P, i_hi_half, SIDE, I_LO]),
+                            op=ALU.mult,
+                        )
+                    nc.vector.tensor_reduce(
+                        out=vectors["sums"][:],
+                        in_=prod[:].rearrange("p (d j i) -> p j d i", j=SIDE, i=I_LO),
+                        axis=AXIS.XY,
+                        op=ALU.add,
+                    )
+                    renew(vectors, "floor_c", "c")
+                for bt in range(BATCH_TILES):
+                    engine = nc.vector if bt < VECTOR_TILES else nc.gpsimd
+                    vectors = state[bt]
+                    prod = work.tile([P, DOUT], F32, name="prod")
+                    for h in range(halves):
+                        engine.tensor_tensor(
+                            out=prod[:, BANK * h : BANK * (h + 1)].rearrange("p (i j) -> p i j", j=SIDE),
+                            in0=by_row[bt][h][:].rearrange("p (i j) -> p i j", j=SIDE),
+                            in1=vectors["c"][:].unsqueeze(1).to_broadcast([P, i_half, SIDE]),
+                            op=ALU.mult,
+                        )
+                    nc.vector.tensor_reduce(
+                        out=vectors["sums"][:],
+                        in_=prod[:].rearrange("p (i j) -> p i j", j=SIDE),
+                        axis=AXIS.X,
+                        op=ALU.add,
+                    )
+                    renew(vectors, "floor_a", "a")
+                    if rnd == ROUNDS - 1:
+                        result = work.tile([P, DOUT], F32, name="result")
+                        engine.tensor_tensor(
+                            out=result[:].rearrange("p (i j) -> p i j", j=SIDE),
+                            in0=prod[:].rearrange("p (i j) -> p i j", j=SIDE),
+                            in1=vectors["a"][:].unsqueeze(2).to_broadcast([P, SIDE, SIDE]),
+                            op=ALU.mult,
+                        )
+                        nc.sync.dma_start(
+                            out=out[P * bt : P * (bt + 1)].rearrange("b i j -> b (i j)"), in_=result[:]
+                        )

@@ -28,6 +28,8 @@ VECTOR_COLS = 512
 I_LO = P // SIDE
 LINEAR_FROM = 30.0
 VECTOR_TILES = 2
+VECTOR_SUMS = 24
+TINY = 1e-30
 
 FLOPS = 2 * BATCH * HID * (HID + DOUT)
 
@@ -198,7 +200,6 @@ def tile_matchingnet_pa_kernel(tc, h3, W4, b4, W5, b5, out):
 
         with ExitStack() as back:
             soft = back.enter_context(tc.tile_pool(name="soft", bufs=1))
-            work = back.enter_context(tc.tile_pool(name="work", bufs=6))
 
             d_tiles = DOUT // P
             expo = soft.tile([P, d_tiles, BATCH], F32, name="expo")
@@ -223,6 +224,9 @@ def tile_matchingnet_pa_kernel(tc, h3, W4, b4, W5, b5, out):
             for bt in reversed(range(BATCH_TILES)):
                 for label, layout, order in (("row", by_row, ident), ("col", by_col, swap)):
                     pieces = []
+                    if bt >= VECTOR_TILES:
+                        in_sbuf = soft.tile([P, DOUT], F32, name="r_%s_%d" % (label, bt))
+                        pieces.append(in_sbuf)
                     for h in range(halves):
                         bank = banks.tile([P, BANK], F32, tag="bank", name="r_bank")
                         for q in range(per_half):
@@ -234,11 +238,11 @@ def tile_matchingnet_pa_kernel(tc, h3, W4, b4, W5, b5, out):
                         if bt < VECTOR_TILES:
                             pieces.append(bank)
                         else:
-                            copy = soft.tile([P, BANK], F32, name="r_%s_%d_%d" % (label, bt, h))
-                            nc.scalar.copy(out=copy[:], in_=bank[:])
-                            pieces.append(copy)
+                            nc.scalar.copy(out=in_sbuf[:, BANK * h : BANK * (h + 1)], in_=bank[:])
                     layout[bt] = pieces
 
+            tiny = soft.tile([P, 1], F32, name="tiny")
+            nc.vector.memset(tiny[:], TINY)
             state = []
             for bt in range(BATCH_TILES):
                 vectors = {}
@@ -246,9 +250,61 @@ def tile_matchingnet_pa_kernel(tc, h3, W4, b4, W5, b5, out):
                     vectors[name] = soft.tile([P, SIDE], F32, name="%s%d" % (name, bt))
                     nc.vector.memset(vectors[name][:], 1.0)
                 vectors["sums"] = soft.tile([P, SIDE], F32, name="sums%d" % bt)
+                vectors["root"] = soft.tile([P, SIDE], F32, name="root%d" % bt)
+                vectors["prod"] = soft.tile([P, DOUT], F32, name="prod%d" % bt)
                 state.append(vectors)
+            for bt in range(BATCH_TILES):
+                state.append({"prod": soft.tile([P, DOUT], F32, name="unused%d" % bt)})
 
-            def renew(vectors, floor, factor):
+            def engine_of(bt):
+                return nc.vector if bt < VECTOR_TILES else nc.gpsimd
+
+            def multiply(bt, step):
+                vectors = state[bt]
+                pieces = by_col[bt] if step % 2 == 0 else by_row[bt]
+                width = DOUT // len(pieces)
+                for h, piece in enumerate(pieces):
+                    part = vectors["prod"][:, width * h : width * (h + 1)]
+                    if step % 2 == 0:
+                        rows = width // SIDE
+                        a_part = vectors["a"][:, rows * h : rows * (h + 1)].rearrange("p (d i) -> p d i", i=I_LO)
+                        engine_of(bt).tensor_tensor(
+                            out=part.rearrange("p (d j i) -> p d j i", j=SIDE, i=I_LO),
+                            in0=piece[:].rearrange("p (d j i) -> p d j i", j=SIDE, i=I_LO),
+                            in1=a_part.unsqueeze(2).to_broadcast([P, rows // I_LO, SIDE, I_LO]),
+                            op=ALU.mult,
+                        )
+                    else:
+                        engine_of(bt).tensor_tensor(
+                            out=part.rearrange("p (i j) -> p i j", j=SIDE),
+                            in0=piece[:].rearrange("p (i j) -> p i j", j=SIDE),
+                            in1=vectors["c"][:].unsqueeze(1).to_broadcast([P, width // SIDE, SIDE]),
+                            op=ALU.mult,
+                        )
+
+            def groups_of(bt, step):
+                prod = state[bt]["prod"][:]
+                if step % 2 == 0:
+                    return prod.rearrange("p (d j i) -> p j d i", j=SIDE, i=I_LO), AXIS.XY
+                return prod.rearrange("p (i j) -> p i j", j=SIDE), AXIS.X
+
+            def add_up_on_vector(bt, step):
+                groups, axis = groups_of(bt, step)
+                nc.vector.tensor_reduce(
+                    out=state[bt]["sums"][:, :VECTOR_SUMS], in_=groups[:, :VECTOR_SUMS], axis=axis, op=ALU.add
+                )
+
+            def add_up_on_scalar(bt, step):
+                groups, axis = groups_of(bt, step)
+                unused, axis = groups_of(bt + BATCH_TILES, step)
+                for s in range(VECTOR_SUMS, SIDE):
+                    nc.scalar.activation(
+                        out=unused[:, s], in_=groups[:, s], func=ACT.Copy, accum_out=state[bt]["sums"][:, s : s + 1]
+                    )
+
+            def renew(bt, step):
+                vectors = state[bt]
+                floor, factor = ("floor_c", "c") if step % 2 == 0 else ("floor_a", "a")
                 nc.vector.scalar_tensor_tensor(
                     out=vectors[floor][:],
                     in0=vectors[floor][:],
@@ -257,56 +313,43 @@ def tile_matchingnet_pa_kernel(tc, h3, W4, b4, W5, b5, out):
                     op0=ALU.mult,
                     op1=ALU.max,
                 )
-                nc.vector.reciprocal(out=vectors[factor][:], in_=vectors[floor][:])
+                nc.scalar.activation(
+                    out=vectors["root"][:], in_=vectors[floor][:], func=ACT.Abs_reciprocal_sqrt, bias=tiny[:], scale=1.0
+                )
+                nc.scalar.activation(out=vectors[factor][:], in_=vectors["root"][:], func=ACT.Square)
 
-            i_hi_half = SIDE // I_LO // halves
-            i_half = SIDE // halves
-            for rnd in range(ROUNDS):
-                for bt in range(BATCH_TILES):
-                    engine = nc.vector if bt < VECTOR_TILES else nc.gpsimd
-                    vectors = state[bt]
-                    prod = work.tile([P, DOUT], F32, name="prod")
-                    for h in range(halves):
-                        a_part = vectors["a"][:, i_half * h : i_half * (h + 1)].rearrange("p (d i) -> p d i", i=I_LO)
-                        engine.tensor_tensor(
-                            out=prod[:, BANK * h : BANK * (h + 1)].rearrange("p (d j i) -> p d j i", j=SIDE, i=I_LO),
-                            in0=by_col[bt][h][:].rearrange("p (d j i) -> p d j i", j=SIDE, i=I_LO),
-                            in1=a_part.unsqueeze(2).to_broadcast([P, i_hi_half, SIDE, I_LO]),
-                            op=ALU.mult,
-                        )
-                    nc.vector.tensor_reduce(
-                        out=vectors["sums"][:],
-                        in_=prod[:].rearrange("p (d j i) -> p j d i", j=SIDE, i=I_LO),
-                        axis=AXIS.XY,
-                        op=ALU.add,
-                    )
-                    renew(vectors, "floor_c", "c")
-                for bt in range(BATCH_TILES):
-                    engine = nc.vector if bt < VECTOR_TILES else nc.gpsimd
-                    vectors = state[bt]
-                    prod = work.tile([P, DOUT], F32, name="prod")
-                    for h in range(halves):
-                        engine.tensor_tensor(
-                            out=prod[:, BANK * h : BANK * (h + 1)].rearrange("p (i j) -> p i j", j=SIDE),
-                            in0=by_row[bt][h][:].rearrange("p (i j) -> p i j", j=SIDE),
-                            in1=vectors["c"][:].unsqueeze(1).to_broadcast([P, i_half, SIDE]),
-                            op=ALU.mult,
-                        )
-                    nc.vector.tensor_reduce(
-                        out=vectors["sums"][:],
-                        in_=prod[:].rearrange("p (i j) -> p i j", j=SIDE),
-                        axis=AXIS.X,
-                        op=ALU.add,
-                    )
-                    renew(vectors, "floor_a", "a")
-                    if rnd == ROUNDS - 1:
-                        result = work.tile([P, DOUT], F32, name="result")
-                        engine.tensor_tensor(
-                            out=result[:].rearrange("p (i j) -> p i j", j=SIDE),
-                            in0=prod[:].rearrange("p (i j) -> p i j", j=SIDE),
-                            in1=vectors["a"][:].unsqueeze(2).to_broadcast([P, SIDE, SIDE]),
-                            op=ALU.mult,
-                        )
-                        nc.sync.dma_start(
-                            out=out[P * bt : P * (bt + 1)].rearrange("b i j -> b (i j)"), in_=result[:]
-                        )
+            def finish(bt):
+                vectors = state[bt]
+                by_matrix = vectors["prod"][:].rearrange("p (i j) -> p i j", j=SIDE)
+                engine_of(bt).tensor_tensor(
+                    out=by_matrix,
+                    in0=by_matrix,
+                    in1=vectors["a"][:].unsqueeze(2).to_broadcast([P, SIDE, SIDE]),
+                    op=ALU.mult,
+                )
+                nc.sync.dma_start(out=out[P * bt : P * (bt + 1)].rearrange("b i j -> b (i j)"), in_=vectors["prod"][:])
+
+            steps = 2 * ROUNDS
+            pairs = [(bt, bt + VECTOR_TILES) for bt in range(VECTOR_TILES)]
+            with tc.manual_schedule():
+                for own, lent in pairs:
+                    multiply(lent, 0)
+                waiting = None
+                for step in range(steps):
+                    for own, lent in pairs:
+                        multiply(own, step)
+                        if waiting is not None:
+                            renew(waiting[0], waiting[1])
+                        add_up_on_scalar(lent, step)
+                        add_up_on_vector(lent, step)
+                        add_up_on_vector(own, step)
+                        renew(lent, step)
+                        add_up_on_scalar(own, step)
+                        if step + 1 < steps:
+                            multiply(lent, step + 1)
+                        else:
+                            finish(lent)
+                        waiting = (own, step)
+                renew(waiting[0], waiting[1])
+                for own, lent in pairs:
+                    finish(own)

@@ -28,7 +28,6 @@ VECTOR_COLS = 512
 I_LO = P // SIDE
 LINEAR_FROM = 30.0
 VECTOR_TILES = 2
-VECTOR_SUMS = 24
 TINY = 1e-30
 
 FLOPS = 2 * BATCH * HID * (HID + DOUT)
@@ -253,8 +252,6 @@ def tile_matchingnet_pa_kernel(tc, h3, W4, b4, W5, b5, out):
                 vectors["root"] = soft.tile([P, SIDE], F32, name="root%d" % bt)
                 vectors["prod"] = soft.tile([P, DOUT], F32, name="prod%d" % bt)
                 state.append(vectors)
-            for bt in range(BATCH_TILES):
-                state.append({"prod": soft.tile([P, DOUT], F32, name="unused%d" % bt)})
 
             def engine_of(bt):
                 return nc.vector if bt < VECTOR_TILES else nc.gpsimd
@@ -282,24 +279,21 @@ def tile_matchingnet_pa_kernel(tc, h3, W4, b4, W5, b5, out):
                             op=ALU.mult,
                         )
 
-            def groups_of(bt, step):
-                prod = state[bt]["prod"][:]
+            def add_up(bt, step):
+                vectors = state[bt]
                 if step % 2 == 0:
-                    return prod.rearrange("p (d j i) -> p j d i", j=SIDE, i=I_LO), AXIS.XY
-                return prod.rearrange("p (i j) -> p i j", j=SIDE), AXIS.X
-
-            def add_up_on_vector(bt, step):
-                groups, axis = groups_of(bt, step)
-                nc.vector.tensor_reduce(
-                    out=state[bt]["sums"][:, :VECTOR_SUMS], in_=groups[:, :VECTOR_SUMS], axis=axis, op=ALU.add
-                )
-
-            def add_up_on_scalar(bt, step):
-                groups, axis = groups_of(bt, step)
-                unused, axis = groups_of(bt + BATCH_TILES, step)
-                for s in range(VECTOR_SUMS, SIDE):
-                    nc.scalar.activation(
-                        out=unused[:, s], in_=groups[:, s], func=ACT.Copy, accum_out=state[bt]["sums"][:, s : s + 1]
+                    nc.vector.tensor_reduce(
+                        out=vectors["sums"][:],
+                        in_=vectors["prod"][:].rearrange("p (d j i) -> p j d i", j=SIDE, i=I_LO),
+                        axis=AXIS.XY,
+                        op=ALU.add,
+                    )
+                else:
+                    nc.vector.tensor_reduce(
+                        out=vectors["sums"][:],
+                        in_=vectors["prod"][:].rearrange("p (i j) -> p i j", j=SIDE),
+                        axis=AXIS.X,
+                        op=ALU.add,
                     )
 
             def renew(bt, step):
@@ -340,11 +334,9 @@ def tile_matchingnet_pa_kernel(tc, h3, W4, b4, W5, b5, out):
                         multiply(own, step)
                         if waiting is not None:
                             renew(waiting[0], waiting[1])
-                        add_up_on_scalar(lent, step)
-                        add_up_on_vector(lent, step)
-                        add_up_on_vector(own, step)
+                        add_up(lent, step)
+                        add_up(own, step)
                         renew(lent, step)
-                        add_up_on_scalar(own, step)
                         if step + 1 < steps:
                             multiply(lent, step + 1)
                         else:

@@ -28,6 +28,7 @@ VECTOR_COLS = 512
 I_LO = P // SIDE
 LINEAR_FROM = 30.0
 VECTOR_TILES = 2
+VECTOR_SUMS = 24
 TINY = 1e-30
 
 FLOPS = 2 * BATCH * HID * (HID + DOUT)
@@ -245,13 +246,17 @@ def tile_matchingnet_pa_kernel(tc, h3, W4, b4, W5, b5, out):
             state = []
             for bt in range(BATCH_TILES):
                 vectors = {}
-                for name in ("a", "c", "floor_a", "floor_c"):
+                for name in ("a", "c"):
                     vectors[name] = soft.tile([P, SIDE], F32, name="%s%d" % (name, bt))
                     nc.vector.memset(vectors[name][:], 1.0)
-                vectors["sums"] = soft.tile([P, SIDE], F32, name="sums%d" % bt)
+                    vectors["bounds_" + name] = soft.tile([P, 2, SIDE], F32, name="bounds_%s%d" % (name, bt))
+                    nc.vector.memset(vectors["bounds_" + name][:, 1, :], EPS)
+                vectors["floor"] = soft.tile([P, SIDE], F32, name="floor%d" % bt)
                 vectors["root"] = soft.tile([P, SIDE], F32, name="root%d" % bt)
                 vectors["prod"] = soft.tile([P, DOUT], F32, name="prod%d" % bt)
                 state.append(vectors)
+            for bt in range(BATCH_TILES):
+                state.append({"prod": soft.tile([P, DOUT], F32, name="unused%d" % bt)})
 
             def engine_of(bt):
                 return nc.vector if bt < VECTOR_TILES else nc.gpsimd
@@ -279,38 +284,39 @@ def tile_matchingnet_pa_kernel(tc, h3, W4, b4, W5, b5, out):
                             op=ALU.mult,
                         )
 
-            def add_up(bt, step):
-                vectors = state[bt]
+            def groups_of(bt, step):
+                prod = state[bt]["prod"][:]
                 if step % 2 == 0:
-                    nc.vector.tensor_reduce(
-                        out=vectors["sums"][:],
-                        in_=vectors["prod"][:].rearrange("p (d j i) -> p j d i", j=SIDE, i=I_LO),
-                        axis=AXIS.XY,
-                        op=ALU.add,
-                    )
-                else:
-                    nc.vector.tensor_reduce(
-                        out=vectors["sums"][:],
-                        in_=vectors["prod"][:].rearrange("p (i j) -> p i j", j=SIDE),
-                        axis=AXIS.X,
-                        op=ALU.add,
-                    )
+                    return prod.rearrange("p (d j i) -> p j d i", j=SIDE, i=I_LO), AXIS.XY
+                return prod.rearrange("p (i j) -> p i j", j=SIDE), AXIS.X
+
+            def factor_of(step):
+                return "c" if step % 2 == 0 else "a"
+
+            def add_up_on_vector(bt, step):
+                groups, axis = groups_of(bt, step)
+                sums = state[bt]["bounds_" + factor_of(step)][:, 0, :]
+                nc.vector.tensor_reduce(out=sums[:, :VECTOR_SUMS], in_=groups[:, :VECTOR_SUMS], axis=axis, op=ALU.add)
+
+            def add_up_on_scalar(bt, step):
+                groups, axis = groups_of(bt, step)
+                unused, axis = groups_of(bt + BATCH_TILES, step)
+                sums = state[bt]["bounds_" + factor_of(step)][:, 0, :]
+                for s in range(VECTOR_SUMS, SIDE):
+                    nc.scalar.activation(out=unused[:, s], in_=groups[:, s], func=ACT.Copy, accum_out=sums[:, s : s + 1])
 
             def renew(bt, step):
                 vectors = state[bt]
-                floor, factor = ("floor_c", "c") if step % 2 == 0 else ("floor_a", "a")
-                nc.vector.scalar_tensor_tensor(
-                    out=vectors[floor][:],
-                    in0=vectors[floor][:],
-                    scalar=EPS,
-                    in1=vectors["sums"][:],
-                    op0=ALU.mult,
-                    op1=ALU.max,
+                factor = factor_of(step)
+                bounds = vectors["bounds_" + factor]
+                nc.vector.tensor_reduce(
+                    out=vectors["floor"][:], in_=bounds[:].rearrange("p t s -> p s t"), axis=AXIS.X, op=ALU.max
                 )
                 nc.scalar.activation(
-                    out=vectors["root"][:], in_=vectors[floor][:], func=ACT.Abs_reciprocal_sqrt, bias=tiny[:], scale=1.0
+                    out=vectors["root"][:], in_=vectors["floor"][:], func=ACT.Abs_reciprocal_sqrt, bias=tiny[:], scale=1.0
                 )
                 nc.scalar.activation(out=vectors[factor][:], in_=vectors["root"][:], func=ACT.Square)
+                nc.scalar.mul(out=bounds[:, 1, :], in_=vectors["floor"][:], mul=EPS)
 
             def finish(bt):
                 vectors = state[bt]
@@ -334,9 +340,11 @@ def tile_matchingnet_pa_kernel(tc, h3, W4, b4, W5, b5, out):
                         multiply(own, step)
                         if waiting is not None:
                             renew(waiting[0], waiting[1])
-                        add_up(lent, step)
-                        add_up(own, step)
+                        add_up_on_scalar(lent, step)
+                        add_up_on_vector(lent, step)
+                        add_up_on_vector(own, step)
                         renew(lent, step)
+                        add_up_on_scalar(own, step)
                         if step + 1 < steps:
                             multiply(lent, step + 1)
                         else:

@@ -22,37 +22,33 @@ EPS = 1e-8
 PASSES = HID // K_PASS
 BATCH_TILES = BATCH // P
 BANK = 512
+BANKS = 8
 W_CHUNK = 1024
+CHUNK_TILES = W_CHUNK // P
+AHEAD = 3
 RUN = 4
-VECTOR_COLS = 512
+VECTOR_COLS = 448
 I_LO = P // SIDE
+D_TILES = DOUT // P
+HALVES = DOUT // BANK
 LINEAR_FROM = 30.0
-VECTOR_TILES = 2
+OWN_TILES = 2
 VECTOR_SUMS = 24
-TINY = 1e-30
+TINY = 1e-24
 
 FLOPS = 2 * BATCH * HID * (HID + DOUT)
-
-
-def regroup(nc, stage, raw):
-    grouped = stage.tile([P, W_CHUNK, PACK], BF16, align_bytes=64, name="grouped")
-    src = raw[:].rearrange("p t (c i) -> p c t i", i=RUN)
-    dst = grouped[:].rearrange("p (c i) t -> p c t i", i=RUN)
-    cut = VECTOR_COLS // RUN
-    nc.vector.tensor_copy(out=dst[:, :cut], in_=src[:, :cut])
-    nc.scalar.copy(out=dst[:, cut:], in_=src[:, cut:])
-    return grouped
-
-
-def quantise(nc, grouped, codes, scales):
-    nc.vector.quantize_mx(out=codes.bitcast(FP8X4), scales=scales, in_=grouped)
 
 
 def tile_matchingnet_pa_kernel(tc, h3, W4, b4, W5, b5, out):
     nc = tc.nc
     with ExitStack() as whole:
         consts = whole.enter_context(tc.tile_pool(name="consts", bufs=1))
-        banks = whole.enter_context(tc.psum_pool(name="banks", bufs=8))
+        banks = whole.enter_context(tc.psum_pool(name="banks", bufs=BANKS))
+
+        tiny = consts.tile([P, 1], F32, name="tiny")
+        nc.vector.memset(tiny[:], TINY)
+        warm = consts.tile([P, 1], F32, name="warm")
+        nc.scalar.activation(out=warm[:], in_=tiny[:], func=ACT.Exp)
 
         ident = consts.tile([P, P], F32, name="ident")
         make_identity(nc, ident[:])
@@ -62,36 +58,43 @@ def tile_matchingnet_pa_kernel(tc, h3, W4, b4, W5, b5, out):
             in_=ident[:].rearrange("p (i j) -> p j i", i=I_LO),
         )
 
-        b4_rows = HID // P
-        b5_rows = DOUT // P
-        bias_rows = consts.tile([P, P], BF16, name="bias_rows")
-        nc.vector.memset(bias_rows[:], 0.0)
-        nc.scalar.dma_start(out=bias_rows[0:b4_rows, :], in_=b4.rearrange("(r c) -> r c", c=P))
-        nc.scalar.dma_start(
-            out=bias_rows[b4_rows : b4_rows + b5_rows, :], in_=b5.rearrange("(r c) -> r c", c=P)
-        )
-        bias_rows_f32 = consts.tile([P, P], F32, name="bias_rows_f32")
-        nc.vector.tensor_copy(out=bias_rows_f32[:], in_=bias_rows[:])
-        bias_bank = banks.tile([P, P], F32, tag="bank", name="bias_bank")
-        nc.tensor.transpose(bias_bank[:], bias_rows_f32[:], ident[:])
-        bias_cols = consts.tile([P, b4_rows + b5_rows], F32, name="bias_cols")
-        nc.vector.tensor_copy(out=bias_cols[:], in_=bias_bank[:, 0 : b4_rows + b5_rows])
-
         z_banks = []
         with ExitStack() as front:
             keep = front.enter_context(tc.tile_pool(name="keep", bufs=1))
-            wraw = front.enter_context(tc.tile_pool(name="wraw", bufs=4))
+            wraw = front.enter_context(tc.tile_pool(name="wraw", bufs=AHEAD + 1))
             stage = front.enter_context(tc.tile_pool(name="stage", bufs=3))
             acts = front.enter_context(tc.tile_pool(name="acts", bufs=2))
 
-            h3_rows = []
+            chunks = [("w4", block, g) for block in range(HID // W_CHUNK) for g in range(PASSES)]
+            chunks += [("w5", 0, g) for g in range(PASSES)]
+            raws = {}
+
+            def load(c):
+                weights, block, g = chunks[c]
+                raw = wraw.tile([P, PACK, W_CHUNK], BF16, name="raw")
+                cols = slice(W_CHUNK * block, W_CHUNK * (block + 1))
+                if weights == "w4":
+                    for u in range(2):
+                        first = K_PASS * g + (K_PASS // 2) * u
+                        rows = W4[first : first + K_PASS // 2, cols]
+                        nc.sync.dma_start(
+                            out=raw[:, 2 * u : 2 * u + 2, :], in_=rows.rearrange("(q e) c -> q e c", e=2)
+                        )
+                else:
+                    rows = W5[K_PASS * g : K_PASS * (g + 1), cols]
+                    nc.sync.dma_start(out=raw[:], in_=rows.rearrange("(t p) n -> p t n", p=P))
+                raws[c] = raw
+
+            h3_rows = [keep.tile([P, HID], BF16, name="h3_rows%d" % bt) for bt in range(BATCH_TILES)]
             for bt in range(BATCH_TILES):
-                rows = keep.tile([P, HID], BF16, name="h3_rows%d" % bt)
-                nc.sync.dma_start(out=rows[:], in_=h3[bt * P : (bt + 1) * P, :])
-                h3_rows.append(rows)
+                nc.sync.dma_start(out=h3_rows[bt][:], in_=h3[bt * P : (bt + 1) * P, :])
+                if bt == BATCH_TILES // 2 - 1:
+                    load(0)
+            for c in range(1, AHEAD):
+                load(c)
+
             h3_grouped = [
-                keep.tile([P, BATCH * PACK], BF16, align_bytes=64, name="h3_grouped%d" % g)
-                for g in range(PASSES)
+                keep.tile([P, BATCH * PACK], BF16, align_bytes=64, name="h3_grouped%d" % g) for g in range(PASSES)
             ]
             h3_codes = keep.tile([P, PASSES, BATCH], U32, align_bytes=64, name="h3_codes")
             h3_scales = keep.tile([P, PASSES, BATCH], U8, align_bytes=64, name="h3_scales")
@@ -115,61 +118,74 @@ def tile_matchingnet_pa_kernel(tc, h3, W4, b4, W5, b5, out):
                     else:
                         nc.scalar.copy(out=dst, in_=src)
             for g in range(PASSES):
-                quantise(nc, h3_grouped[g][:], h3_codes[:, g, :], h3_scales[:, g, :])
+                nc.vector.quantize_mx(
+                    out=h3_codes[:, g, :].bitcast(FP8X4), scales=h3_scales[:, g, :], in_=h3_grouped[g][:]
+                )
 
-            w4_codes = keep.tile([P, PASSES, HID], U32, align_bytes=64, name="w4_codes")
-            w4_scales = keep.tile([P, PASSES, HID], U8, align_bytes=64, name="w4_scales")
-            w5_codes = keep.tile([P, PASSES, DOUT], U32, align_bytes=64, name="w5_codes")
-            w5_scales = keep.tile([P, PASSES, DOUT], U8, align_bytes=64, name="w5_scales")
+            b4_rows = HID // P
+            bias_rows = consts.tile([P, P], BF16, name="bias_rows")
+            nc.vector.memset(bias_rows[:], 0.0)
+            nc.sync.dma_start(out=bias_rows[0:b4_rows, :], in_=b4.rearrange("(r c) -> r c", c=P))
+            nc.sync.dma_start(out=bias_rows[b4_rows : b4_rows + D_TILES, :], in_=b5.rearrange("(r c) -> r c", c=P))
+            bias_rows_f32 = consts.tile([P, P], F32, name="bias_rows_f32")
+            nc.vector.tensor_copy(out=bias_rows_f32[:], in_=bias_rows[:])
+            bias_bank = banks.tile([P, P], F32, tag="bank", name="bias_bank")
+            nc.tensor.transpose(bias_bank[:], bias_rows_f32[:], ident[:])
+            bias_cols = consts.tile([P, b4_rows + D_TILES], F32, name="bias_cols")
+            nc.vector.tensor_copy(out=bias_cols[:], in_=bias_bank[:, 0 : b4_rows + D_TILES])
+
+            w_codes = {
+                "w4": keep.tile([P, PASSES, HID], U32, align_bytes=64, name="w4_codes"),
+                "w5": keep.tile([P, PASSES, DOUT], U32, align_bytes=64, name="w5_codes"),
+            }
+            w_scales = {
+                "w4": keep.tile([P, PASSES, HID], U8, align_bytes=64, name="w4_scales"),
+                "w5": keep.tile([P, PASSES, DOUT], U8, align_bytes=64, name="w5_scales"),
+            }
             h4_codes = keep.tile([P, PASSES, BATCH], U32, align_bytes=64, name="h4_codes")
             h4_scales = keep.tile([P, PASSES, BATCH], U8, align_bytes=64, name="h4_scales")
+            moving = {"w4": (h3_codes, h3_scales), "w5": (h4_codes, h4_scales)}
 
-            def load_w4(block, g):
-                raw = wraw.tile([P, PACK, W_CHUNK], BF16, name="raw")
-                for u in range(2):
-                    first = K_PASS * g + (K_PASS // 2) * u
-                    rows = W4[first : first + K_PASS // 2, W_CHUNK * block : W_CHUNK * (block + 1)]
-                    nc.sync.dma_start(
-                        out=raw[:, 2 * u : 2 * u + 2, :], in_=rows.rearrange("(q e) c -> q e c", e=2)
-                    )
-                return raw
+            groupeds = {}
 
-            def load_w5(g):
-                raw = wraw.tile([P, PACK, W_CHUNK], BF16, name="raw")
-                rows = W5[K_PASS * g : K_PASS * (g + 1), :]
-                nc.sync.dma_start(out=raw[:], in_=rows.rearrange("(t p) n -> p t n", p=P))
-                return raw
+            def regroup(c):
+                grouped = stage.tile([P, W_CHUNK, PACK], BF16, align_bytes=64, name="grouped")
+                src = raws[c][:].rearrange("p t (c i) -> p c t i", i=RUN)
+                dst = grouped[:].rearrange("p (c i) t -> p c t i", i=RUN)
+                cut = VECTOR_COLS // RUN
+                nc.vector.tensor_copy(out=dst[:, :cut], in_=src[:, :cut])
+                nc.scalar.copy(out=dst[:, cut:], in_=src[:, cut:])
+                groupeds[c] = grouped
 
-            tiles_per_block = W_CHUNK // P
-            for block in range(HID // W_CHUNK):
-                h4_banks = [
-                    banks.tile([P, BANK], F32, tag="bank", name="h4_bank%d" % m) for m in range(tiles_per_block)
-                ]
+            def quantise_and_multiply(c, sums_banks):
+                weights, block, g = chunks[c]
                 cols = slice(W_CHUNK * block, W_CHUNK * (block + 1))
-                for g in range(PASSES):
-                    grouped = regroup(nc, stage, load_w4(block, g))
-                    quantise(
-                        nc, grouped[:].rearrange("p w t -> p (w t)"), w4_codes[:, g, cols], w4_scales[:, g, cols]
+                nc.vector.quantize_mx(
+                    out=w_codes[weights][:, g, cols].bitcast(FP8X4),
+                    scales=w_scales[weights][:, g, cols],
+                    in_=groupeds[c][:].rearrange("p w t -> p (w t)"),
+                )
+                for m in range(CHUNK_TILES):
+                    first = W_CHUNK * block + P * m
+                    nc.tensor.matmul_mx(
+                        out=sums_banks[m][:],
+                        lhsT=w_codes[weights][:, g, first : first + P].bitcast(FP8X4),
+                        lhsT_scale=w_scales[weights][:, g, first : first + P],
+                        rhs=moving[weights][0][:, g, :].bitcast(FP8X4),
+                        rhs_scale=moving[weights][1][:, g, :],
+                        start=(g == 0),
+                        stop=(g == PASSES - 1),
                     )
-                    for m in range(tiles_per_block):
-                        first = W_CHUNK * block + P * m
-                        nc.tensor.matmul_mx(
-                            out=h4_banks[m][:],
-                            lhsT=w4_codes[:, g, first : first + P].bitcast(FP8X4),
-                            lhsT_scale=w4_scales[:, g, first : first + P],
-                            rhs=h3_codes[:, g, :].bitcast(FP8X4),
-                            rhs_scale=h3_scales[:, g, :],
-                            start=(g == 0),
-                            stop=(g == PASSES - 1),
-                        )
-                for quad in range(tiles_per_block // PACK):
-                    g2 = (tiles_per_block // PACK) * block + quad
+
+            def activate(block, sums_banks):
+                for quad in range(CHUNK_TILES // PACK):
+                    g2 = (CHUNK_TILES // PACK) * block + quad
                     biased = acts.tile([P, PACK, BATCH], F32, name="biased")
                     for t in range(PACK):
                         m = PACK * g2 + t
                         nc.scalar.activation(
                             out=biased[:, t, :],
-                            in_=h4_banks[PACK * quad + t][:],
+                            in_=sums_banks[PACK * quad + t][:],
                             func=ACT.Identity,
                             bias=bias_cols[:, m : m + 1],
                             scale=1.0,
@@ -179,70 +195,83 @@ def tile_matchingnet_pa_kernel(tc, h3, W4, b4, W5, b5, out):
                     nc.vector.scalar_tensor_tensor(
                         out=h4_grouped[:], in0=by_column, scalar=SLOPE, in1=by_column, op0=ALU.mult, op1=ALU.max
                     )
-                    quantise(
-                        nc, h4_grouped[:].rearrange("p b t -> p (b t)"), h4_codes[:, g2, :], h4_scales[:, g2, :]
+                    nc.vector.quantize_mx(
+                        out=h4_codes[:, g2, :].bitcast(FP8X4),
+                        scales=h4_scales[:, g2, :],
+                        in_=h4_grouped[:].rearrange("p b t -> p (b t)"),
                     )
 
-            z_banks = [banks.tile([P, BANK], F32, tag="bank", name="z_bank%d" % d) for d in range(DOUT // P)]
-            for g in range(PASSES):
-                grouped = regroup(nc, stage, load_w5(g))
-                quantise(nc, grouped[:].rearrange("p w t -> p (w t)"), w5_codes[:, g, :], w5_scales[:, g, :])
-                for d in range(DOUT // P):
-                    nc.tensor.matmul_mx(
-                        out=z_banks[d][:],
-                        lhsT=w5_codes[:, g, P * d : P * (d + 1)].bitcast(FP8X4),
-                        lhsT_scale=w5_scales[:, g, P * d : P * (d + 1)],
-                        rhs=h4_codes[:, g, :].bitcast(FP8X4),
-                        rhs_scale=h4_scales[:, g, :],
-                        start=(g == 0),
-                        stop=(g == PASSES - 1),
-                    )
+            sums_banks = []
+            for c in range(len(chunks) + 1):
+                if c + AHEAD < len(chunks):
+                    load(c + AHEAD)
+                if c < len(chunks):
+                    regroup(c)
+                if c > 0:
+                    weights, block, g = chunks[c - 1]
+                    if g == 0:
+                        sums_banks = [
+                            banks.tile([P, BANK], F32, tag="bank", name="sums_bank%d" % m) for m in range(CHUNK_TILES)
+                        ]
+                    quantise_and_multiply(c - 1, sums_banks)
+                    if weights == "w4" and g == PASSES - 1:
+                        activate(block, sums_banks)
+            z_banks = sums_banks
 
         with ExitStack() as back:
             soft = back.enter_context(tc.tile_pool(name="soft", bufs=1))
 
-            d_tiles = DOUT // P
-            expo = soft.tile([P, d_tiles, BATCH], F32, name="expo")
-            r_flipped = soft.tile([P, d_tiles, BATCH], F32, name="r_flipped")
-            for d in range(d_tiles):
+            expo = soft.tile([P, D_TILES, BATCH], F32, name="expo")
+            r_flipped = soft.tile([P, D_TILES, BATCH], F32, name="r_flipped")
+            for d in range(D_TILES):
                 b5_col = bias_cols[:, b4_rows + d : b4_rows + d + 1]
                 nc.vector.tensor_scalar(
                     out=expo[:, d, :], in0=z_banks[d][:], scalar1=b5_col, scalar2=LINEAR_FROM, op0=ALU.add, op1=ALU.min
                 )
                 nc.scalar.activation(out=expo[:, d, :], in_=expo[:, d, :], func=ACT.Exp)
-            for d in range(d_tiles):
-                b5_col = bias_cols[:, b4_rows + d : b4_rows + d + 1]
-                nc.scalar.activation(out=expo[:, d, :], in_=expo[:, d, :], func=ACT.Ln, bias=1.0, scale=1.0)
-                nc.vector.scalar_tensor_tensor(
-                    out=r_flipped[:, d, :], in0=z_banks[d][:], scalar=b5_col, in1=expo[:, d, :], op0=ALU.add, op1=ALU.max
-                )
 
-            halves = DOUT // BANK
+            own_tiles = range(OWN_TILES)
+            lent_tiles = range(OWN_TILES, BATCH_TILES)
+            orders = {"col": swap, "row": ident}
+            matrices = {"col": {}, "row": {}}
             per_half = BANK // P
-            by_row = {}
-            by_col = {}
-            for bt in reversed(range(BATCH_TILES)):
-                for label, layout, order in (("row", by_row, ident), ("col", by_col, swap)):
-                    pieces = []
-                    if bt >= VECTOR_TILES:
-                        in_sbuf = soft.tile([P, DOUT], F32, name="r_%s_%d" % (label, bt))
-                        pieces.append(in_sbuf)
-                    for h in range(halves):
-                        bank = banks.tile([P, BANK], F32, tag="bank", name="r_bank")
-                        for q in range(per_half):
-                            nc.tensor.transpose(
-                                bank[:, P * q : P * (q + 1)],
-                                r_flipped[:, per_half * h + q, P * bt : P * (bt + 1)],
-                                order[:],
-                            )
-                        if bt < VECTOR_TILES:
-                            pieces.append(bank)
-                        else:
-                            nc.scalar.copy(out=in_sbuf[:, BANK * h : BANK * (h + 1)], in_=bank[:])
-                    layout[bt] = pieces
 
-            tiny = soft.tile([P, 1], F32, name="tiny")
-            nc.vector.memset(tiny[:], TINY)
+            def flip_back(label, bt, h):
+                bank = banks.tile([P, BANK], F32, tag="bank", name="r_bank")
+                for q in range(per_half):
+                    nc.tensor.transpose(
+                        bank[:, P * q : P * (q + 1)],
+                        r_flipped[:, per_half * h + q, P * bt : P * (bt + 1)],
+                        orders[label][:],
+                    )
+                return bank
+
+            for label in ("col", "row"):
+                for bt in lent_tiles:
+                    matrices[label][bt] = [soft.tile([P, DOUT], F32, name="r_%s_%d" % (label, bt))]
+            staged = []
+            for h in range(HALVES):
+                for q in range(per_half):
+                    d = per_half * h + q
+                    b5_col = bias_cols[:, b4_rows + d : b4_rows + d + 1]
+                    nc.scalar.activation(out=expo[:, d, :], in_=expo[:, d, :], func=ACT.Ln, bias=1.0, scale=1.0)
+                    nc.vector.scalar_tensor_tensor(
+                        out=r_flipped[:, d, :], in0=z_banks[d][:], scalar=b5_col, in1=expo[:, d, :], op0=ALU.add, op1=ALU.max
+                    )
+                for label in ("col", "row"):
+                    for bt in lent_tiles:
+                        staged.append((label, bt, h, flip_back(label, bt, h)))
+            for label, bt, h, bank in staged:
+                in_sbuf = matrices[label][bt][0][:, BANK * h : BANK * (h + 1)]
+                if label == "col":
+                    nc.vector.tensor_copy(out=in_sbuf, in_=bank[:])
+                else:
+                    nc.scalar.copy(out=in_sbuf, in_=bank[:])
+            for bt in own_tiles:
+                for label in ("col", "row"):
+                    matrices[label][bt] = [flip_back(label, bt, h) for h in range(HALVES)]
+            nc.scalar.activation(out=warm[:], in_=tiny[:], func=ACT.Abs_reciprocal_sqrt)
+
             state = []
             for bt in range(BATCH_TILES):
                 vectors = {}
@@ -254,56 +283,62 @@ def tile_matchingnet_pa_kernel(tc, h3, W4, b4, W5, b5, out):
                 vectors["floor"] = soft.tile([P, SIDE], F32, name="floor%d" % bt)
                 vectors["root"] = soft.tile([P, SIDE], F32, name="root%d" % bt)
                 vectors["prod"] = soft.tile([P, DOUT], F32, name="prod%d" % bt)
+                vectors["unused"] = soft.tile([P, SIDE - VECTOR_SUMS, SIDE], F32, name="unused%d" % bt)
                 state.append(vectors)
-            for bt in range(BATCH_TILES):
-                state.append({"prod": soft.tile([P, DOUT], F32, name="unused%d" % bt)})
 
-            def engine_of(bt):
-                return nc.vector if bt < VECTOR_TILES else nc.gpsimd
+            def factor_of(step):
+                return "c" if step % 2 == 0 else "a"
 
             def multiply(bt, step):
+                engine = nc.vector if bt in own_tiles else nc.gpsimd
                 vectors = state[bt]
-                pieces = by_col[bt] if step % 2 == 0 else by_row[bt]
+                pieces = matrices["col" if step % 2 == 0 else "row"][bt]
                 width = DOUT // len(pieces)
                 for h, piece in enumerate(pieces):
                     part = vectors["prod"][:, width * h : width * (h + 1)]
                     if step % 2 == 0:
                         rows = width // SIDE
                         a_part = vectors["a"][:, rows * h : rows * (h + 1)].rearrange("p (d i) -> p d i", i=I_LO)
-                        engine_of(bt).tensor_tensor(
+                        engine.tensor_tensor(
                             out=part.rearrange("p (d j i) -> p d j i", j=SIDE, i=I_LO),
                             in0=piece[:].rearrange("p (d j i) -> p d j i", j=SIDE, i=I_LO),
                             in1=a_part.unsqueeze(2).to_broadcast([P, rows // I_LO, SIDE, I_LO]),
                             op=ALU.mult,
                         )
                     else:
-                        engine_of(bt).tensor_tensor(
+                        engine.tensor_tensor(
                             out=part.rearrange("p (i j) -> p i j", j=SIDE),
                             in0=piece[:].rearrange("p (i j) -> p i j", j=SIDE),
                             in1=vectors["c"][:].unsqueeze(1).to_broadcast([P, width // SIDE, SIDE]),
                             op=ALU.mult,
                         )
 
-            def groups_of(bt, step):
-                prod = state[bt]["prod"][:]
+            def terms_of(bt, step):
+                if step == 0 and bt in lent_tiles:
+                    terms = matrices["col"][bt][0][:]
+                else:
+                    terms = state[bt]["prod"][:]
                 if step % 2 == 0:
-                    return prod.rearrange("p (d j i) -> p j d i", j=SIDE, i=I_LO), AXIS.XY
-                return prod.rearrange("p (i j) -> p i j", j=SIDE), AXIS.X
+                    return terms.rearrange("p (d j i) -> p j d i", j=SIDE, i=I_LO)
+                return terms.rearrange("p (i j) -> p i j", j=SIDE)
 
-            def factor_of(step):
-                return "c" if step % 2 == 0 else "a"
-
-            def add_up_on_vector(bt, step):
-                groups, axis = groups_of(bt, step)
+            def add_up_on_vector(bt, step, count):
                 sums = state[bt]["bounds_" + factor_of(step)][:, 0, :]
-                nc.vector.tensor_reduce(out=sums[:, :VECTOR_SUMS], in_=groups[:, :VECTOR_SUMS], axis=axis, op=ALU.add)
+                nc.vector.tensor_reduce(
+                    out=sums[:, :count],
+                    in_=terms_of(bt, step)[:, :count],
+                    axis=AXIS.XY if step % 2 == 0 else AXIS.X,
+                    op=ALU.add,
+                )
 
-            def add_up_on_scalar(bt, step):
-                groups, axis = groups_of(bt, step)
-                unused, axis = groups_of(bt + BATCH_TILES, step)
+            def add_up_on_scalar(bt, step, done):
                 sums = state[bt]["bounds_" + factor_of(step)][:, 0, :]
-                for s in range(VECTOR_SUMS, SIDE):
-                    nc.scalar.activation(out=unused[:, s], in_=groups[:, s], func=ACT.Copy, accum_out=sums[:, s : s + 1])
+                terms = terms_of(bt, step)
+                for s in range(done, SIDE):
+                    unused = state[bt]["unused"][:, s - done, :]
+                    if step % 2 == 0:
+                        unused = unused.rearrange("p (d i) -> p d i", i=I_LO)
+                    nc.scalar.activation(out=unused, in_=terms[:, s], func=ACT.Copy, accum_out=sums[:, s : s + 1])
 
             def renew(bt, step):
                 vectors = state[bt]
@@ -318,10 +353,10 @@ def tile_matchingnet_pa_kernel(tc, h3, W4, b4, W5, b5, out):
                 nc.scalar.activation(out=vectors[factor][:], in_=vectors["root"][:], func=ACT.Square)
                 nc.scalar.mul(out=bounds[:, 1, :], in_=vectors["floor"][:], mul=EPS)
 
-            def finish(bt):
+            def finish(bt, engine):
                 vectors = state[bt]
                 by_matrix = vectors["prod"][:].rearrange("p (i j) -> p i j", j=SIDE)
-                engine_of(bt).tensor_tensor(
+                engine.tensor_tensor(
                     out=by_matrix,
                     in0=by_matrix,
                     in1=vectors["a"][:].unsqueeze(2).to_broadcast([P, SIDE, SIDE]),
@@ -330,26 +365,24 @@ def tile_matchingnet_pa_kernel(tc, h3, W4, b4, W5, b5, out):
                 nc.sync.dma_start(out=out[P * bt : P * (bt + 1)].rearrange("b i j -> b (i j)"), in_=vectors["prod"][:])
 
             steps = 2 * ROUNDS
-            pairs = [(bt, bt + VECTOR_TILES) for bt in range(VECTOR_TILES)]
+            pairs = [(bt, bt + OWN_TILES) for bt in own_tiles]
             with tc.manual_schedule():
-                for own, lent in pairs:
-                    multiply(lent, 0)
                 waiting = None
                 for step in range(steps):
                     for own, lent in pairs:
+                        add_up_on_scalar(lent, step, VECTOR_SUMS)
                         multiply(own, step)
                         if waiting is not None:
                             renew(waiting[0], waiting[1])
-                        add_up_on_scalar(lent, step)
-                        add_up_on_vector(lent, step)
-                        add_up_on_vector(own, step)
+                        add_up_on_vector(lent, step, VECTOR_SUMS)
+                        add_up_on_vector(own, step, SIDE)
                         renew(lent, step)
-                        add_up_on_scalar(own, step)
                         if step + 1 < steps:
                             multiply(lent, step + 1)
-                        else:
-                            finish(lent)
+                        elif lent != pairs[-1][1]:
+                            finish(lent, nc.gpsimd)
                         waiting = (own, step)
                 renew(waiting[0], waiting[1])
-                for own, lent in pairs:
-                    finish(own)
+                finish(pairs[0][0], nc.vector)
+                finish(pairs[-1][1], nc.vector)
+                finish(pairs[-1][0], nc.vector)

@@ -28,12 +28,11 @@ CHUNK_TILES = W_CHUNK // P
 AHEAD = 3
 RUN = 4
 VECTOR_COLS = 448
-I_LO = P // SIDE
+LO = P // SIDE
+HI = SIDE // LO
 D_TILES = DOUT // P
 HALVES = DOUT // BANK
 LINEAR_FROM = 30.0
-OWN_TILES = 2
-VECTOR_SUMS = 24
 TINY = 1e-24
 
 FLOPS = 2 * BATCH * HID * (HID + DOUT)
@@ -52,10 +51,16 @@ def tile_matchingnet_pa_kernel(tc, h3, W4, b4, W5, b5, out):
 
         ident = consts.tile([P, P], F32, name="ident")
         make_identity(nc, ident[:])
-        swap = consts.tile([P, P], F32, name="swap")
+        orders = {}
+        for label in ("col", "row"):
+            orders[label] = consts.tile([P, P], F32, name="order_" + label)
         nc.vector.tensor_copy(
-            out=swap[:].rearrange("p (j i) -> p j i", i=I_LO),
-            in_=ident[:].rearrange("p (i j) -> p j i", i=I_LO),
+            out=orders["col"][:].rearrange("p (j i) -> p j i", i=LO),
+            in_=ident[:].rearrange("p (i j) -> p j i", i=LO),
+        )
+        nc.vector.tensor_copy(
+            out=orders["row"][:].rearrange("p (a i l) -> p a i l", i=LO, l=LO),
+            in_=ident[:].rearrange("p (i a l) -> p a i l", i=LO, l=LO),
         )
 
         z_banks = []
@@ -230,13 +235,12 @@ def tile_matchingnet_pa_kernel(tc, h3, W4, b4, W5, b5, out):
                 )
                 nc.scalar.activation(out=expo[:, d, :], in_=expo[:, d, :], func=ACT.Exp)
 
-            own_tiles = range(OWN_TILES)
-            lent_tiles = range(OWN_TILES, BATCH_TILES)
-            orders = {"col": swap, "row": ident}
-            matrices = {"col": {}, "row": {}}
+            matrices = {}
+            for label in ("col", "row"):
+                matrices[label] = [soft.tile([P, DOUT], F32, name="r_%s_%d" % (label, bt)) for bt in range(BATCH_TILES)]
             per_half = BANK // P
 
-            def flip_back(label, bt, h):
+            def flip_back(label, bt, h, engine_copy):
                 bank = banks.tile([P, BANK], F32, tag="bank", name="r_bank")
                 for q in range(per_half):
                     nc.tensor.transpose(
@@ -244,12 +248,16 @@ def tile_matchingnet_pa_kernel(tc, h3, W4, b4, W5, b5, out):
                         r_flipped[:, per_half * h + q, P * bt : P * (bt + 1)],
                         orders[label][:],
                     )
-                return bank
+                if label == "col":
+                    engine_copy(out=matrices[label][bt][:, BANK * h : BANK * (h + 1)], in_=bank[:])
+                else:
+                    engine_copy(
+                        out=matrices[label][bt][:].rearrange("p (a d x) -> p d a x", a=HI, d=HI)[
+                            :, per_half * h : per_half * (h + 1)
+                        ],
+                        in_=bank[:].rearrange("p (d a x) -> p d a x", d=per_half, a=HI),
+                    )
 
-            for label in ("col", "row"):
-                for bt in lent_tiles:
-                    matrices[label][bt] = [soft.tile([P, DOUT], F32, name="r_%s_%d" % (label, bt))]
-            staged = []
             for h in range(HALVES):
                 for q in range(per_half):
                     d = per_half * h + q
@@ -258,18 +266,10 @@ def tile_matchingnet_pa_kernel(tc, h3, W4, b4, W5, b5, out):
                     nc.vector.scalar_tensor_tensor(
                         out=r_flipped[:, d, :], in0=z_banks[d][:], scalar=b5_col, in1=expo[:, d, :], op0=ALU.add, op1=ALU.max
                     )
-                for label in ("col", "row"):
-                    for bt in lent_tiles:
-                        staged.append((label, bt, h, flip_back(label, bt, h)))
-            for label, bt, h, bank in staged:
-                in_sbuf = matrices[label][bt][0][:, BANK * h : BANK * (h + 1)]
-                if label == "col":
-                    nc.vector.tensor_copy(out=in_sbuf, in_=bank[:])
-                else:
-                    nc.scalar.copy(out=in_sbuf, in_=bank[:])
-            for bt in own_tiles:
-                for label in ("col", "row"):
-                    matrices[label][bt] = [flip_back(label, bt, h) for h in range(HALVES)]
+            for label in ("col", "row"):
+                for bt in range(BATCH_TILES):
+                    flip_back(label, bt, 0, nc.vector.tensor_copy)
+                    flip_back(label, bt, 1, nc.scalar.copy)
             nc.scalar.activation(out=warm[:], in_=tiny[:], func=ACT.Abs_reciprocal_sqrt)
 
             state = []
@@ -277,112 +277,105 @@ def tile_matchingnet_pa_kernel(tc, h3, W4, b4, W5, b5, out):
                 vectors = {}
                 for name in ("a", "c"):
                     vectors[name] = soft.tile([P, SIDE], F32, name="%s%d" % (name, bt))
-                    nc.vector.memset(vectors[name][:], 1.0)
-                    vectors["bounds_" + name] = soft.tile([P, 2, SIDE], F32, name="bounds_%s%d" % (name, bt))
-                    nc.vector.memset(vectors["bounds_" + name][:, 1, :], EPS)
-                vectors["floor"] = soft.tile([P, SIDE], F32, name="floor%d" % bt)
+                    vectors["floor_" + name] = soft.tile([P, SIDE], F32, name="floor_%s%d" % (name, bt))
+                    nc.vector.memset(vectors["floor_" + name][:], 1.0)
+                vectors["sums"] = soft.tile([P, SIDE], F32, name="sums%d" % bt)
                 vectors["root"] = soft.tile([P, SIDE], F32, name="root%d" % bt)
                 vectors["prod"] = soft.tile([P, DOUT], F32, name="prod%d" % bt)
-                vectors["unused"] = soft.tile([P, SIDE - VECTOR_SUMS, SIDE], F32, name="unused%d" % bt)
+                vectors["partial"] = soft.tile([P, P], F32, name="partial%d" % bt)
                 state.append(vectors)
 
-            def factor_of(step):
+            def label_of(step):
+                return "col" if step % 2 == 0 else "row"
+
+            def old_factor(step):
+                return "a" if step % 2 == 0 else "c"
+
+            def new_factor(step):
                 return "c" if step % 2 == 0 else "a"
 
-            def multiply(bt, step):
-                engine = nc.vector if bt in own_tiles else nc.gpsimd
-                vectors = state[bt]
-                pieces = matrices["col" if step % 2 == 0 else "row"][bt]
-                width = DOUT // len(pieces)
-                for h, piece in enumerate(pieces):
-                    part = vectors["prod"][:, width * h : width * (h + 1)]
-                    if step % 2 == 0:
-                        rows = width // SIDE
-                        a_part = vectors["a"][:, rows * h : rows * (h + 1)].rearrange("p (d i) -> p d i", i=I_LO)
-                        engine.tensor_tensor(
-                            out=part.rearrange("p (d j i) -> p d j i", j=SIDE, i=I_LO),
-                            in0=piece[:].rearrange("p (d j i) -> p d j i", j=SIDE, i=I_LO),
-                            in1=a_part.unsqueeze(2).to_broadcast([P, rows // I_LO, SIDE, I_LO]),
-                            op=ALU.mult,
-                        )
-                    else:
-                        engine.tensor_tensor(
-                            out=part.rearrange("p (i j) -> p i j", j=SIDE),
-                            in0=piece[:].rearrange("p (i j) -> p i j", j=SIDE),
-                            in1=vectors["c"][:].unsqueeze(1).to_broadcast([P, width // SIDE, SIDE]),
-                            op=ALU.mult,
-                        )
+            def spread(vector):
+                return vector[:].rearrange("p (d l) -> p d l", l=LO).unsqueeze(2).to_broadcast([P, HI, SIDE, LO])
 
             def terms_of(bt, step):
-                if step == 0 and bt in lent_tiles:
-                    terms = matrices["col"][bt][0][:]
-                else:
-                    terms = state[bt]["prod"][:]
-                if step % 2 == 0:
-                    return terms.rearrange("p (d j i) -> p j d i", j=SIDE, i=I_LO)
-                return terms.rearrange("p (i j) -> p i j", j=SIDE)
+                return matrices["col"][bt] if step == 0 else state[bt]["prod"]
 
-            def add_up_on_vector(bt, step, count):
-                sums = state[bt]["bounds_" + factor_of(step)][:, 0, :]
-                nc.vector.tensor_reduce(
-                    out=sums[:, :count],
-                    in_=terms_of(bt, step)[:, :count],
-                    axis=AXIS.XY if step % 2 == 0 else AXIS.X,
-                    op=ALU.add,
-                )
+            def multiply(bt, step):
+                for blocks in (slice(0, HI // 2), slice(HI // 2, HI)):
+                    nc.vector.tensor_tensor(
+                        out=state[bt]["prod"][:].rearrange("p (d m l) -> p d m l", m=SIDE, l=LO)[:, blocks],
+                        in0=matrices[label_of(step)][bt][:].rearrange("p (d m l) -> p d m l", m=SIDE, l=LO)[:, blocks],
+                        in1=spread(state[bt][old_factor(step)])[:, blocks],
+                        op=ALU.mult,
+                    )
 
-            def add_up_on_scalar(bt, step, done):
-                sums = state[bt]["bounds_" + factor_of(step)][:, 0, :]
-                terms = terms_of(bt, step)
-                for s in range(done, SIDE):
-                    unused = state[bt]["unused"][:, s - done, :]
-                    if step % 2 == 0:
-                        unused = unused.rearrange("p (d i) -> p d i", i=I_LO)
-                    nc.scalar.activation(out=unused, in_=terms[:, s], func=ACT.Copy, accum_out=sums[:, s : s + 1])
+            folded_banks = {}
+            upright_banks = {}
+
+            def add_blocks(bt, step, blocks):
+                if blocks[0] == 0:
+                    folded_banks[bt] = banks.tile([P, P], F32, tag="bank", name="folded")
+                for d in blocks:
+                    nc.tensor.matmul(
+                        out=folded_banks[bt][:],
+                        lhsT=terms_of(bt, step)[:, P * d : P * (d + 1)],
+                        rhs=ident[:],
+                        start=(d == 0),
+                        stop=(d == HI - 1),
+                        is_transpose=True,
+                    )
+
+            def copy_out(bt):
+                nc.scalar.copy(out=state[bt]["partial"][:], in_=folded_banks[bt][:])
+
+            def flip_sums(bt):
+                upright = banks.tile([P, P], F32, tag="bank", name="upright")
+                nc.tensor.transpose(upright[:], state[bt]["partial"][:], ident[:])
+                upright_banks[bt] = upright
 
             def renew(bt, step):
                 vectors = state[bt]
-                factor = factor_of(step)
-                bounds = vectors["bounds_" + factor]
+                factor = new_factor(step)
+                floor = vectors["floor_" + factor]
                 nc.vector.tensor_reduce(
-                    out=vectors["floor"][:], in_=bounds[:].rearrange("p t s -> p s t"), axis=AXIS.X, op=ALU.max
+                    out=vectors["sums"][:],
+                    in_=upright_banks[bt][:].rearrange("p (m l) -> p m l", l=LO),
+                    axis=AXIS.X,
+                    op=ALU.add,
+                )
+                nc.vector.scalar_tensor_tensor(
+                    out=floor[:], in0=floor[:], scalar=EPS, in1=vectors["sums"][:], op0=ALU.mult, op1=ALU.max
                 )
                 nc.scalar.activation(
-                    out=vectors["root"][:], in_=vectors["floor"][:], func=ACT.Abs_reciprocal_sqrt, bias=tiny[:], scale=1.0
+                    out=vectors["root"][:], in_=floor[:], func=ACT.Abs_reciprocal_sqrt, bias=tiny[:], scale=1.0
                 )
                 nc.scalar.activation(out=vectors[factor][:], in_=vectors["root"][:], func=ACT.Square)
-                nc.scalar.mul(out=bounds[:, 1, :], in_=vectors["floor"][:], mul=EPS)
 
-            def finish(bt, engine):
+            def finish(bt):
                 vectors = state[bt]
-                by_matrix = vectors["prod"][:].rearrange("p (i j) -> p i j", j=SIDE)
-                engine.tensor_tensor(
-                    out=by_matrix,
-                    in0=by_matrix,
-                    in1=vectors["a"][:].unsqueeze(2).to_broadcast([P, SIDE, SIDE]),
+                result = soft.tile([P, DOUT], F32, name="result%d" % bt)
+                nc.vector.tensor_tensor(
+                    out=result[:].rearrange("p (i a l) -> p i a l", a=HI, l=LO),
+                    in0=vectors["prod"][:].rearrange("p (a i l) -> p i a l", a=HI, l=LO),
+                    in1=vectors["a"][:].unsqueeze(2).unsqueeze(3).to_broadcast([P, SIDE, HI, LO]),
                     op=ALU.mult,
                 )
-                nc.sync.dma_start(out=out[P * bt : P * (bt + 1)].rearrange("b i j -> b (i j)"), in_=vectors["prod"][:])
+                nc.sync.dma_start(out=out[P * bt : P * (bt + 1)].rearrange("b i j -> b (i j)"), in_=result[:])
 
-            steps = 2 * ROUNDS
-            pairs = [(bt, bt + OWN_TILES) for bt in own_tiles]
+            turns = 2 * ROUNDS * BATCH_TILES
             with tc.manual_schedule():
-                waiting = None
-                for step in range(steps):
-                    for own, lent in pairs:
-                        add_up_on_scalar(lent, step, VECTOR_SUMS)
-                        multiply(own, step)
-                        if waiting is not None:
-                            renew(waiting[0], waiting[1])
-                        add_up_on_vector(lent, step, VECTOR_SUMS)
-                        add_up_on_vector(own, step, SIDE)
-                        renew(lent, step)
-                        if step + 1 < steps:
-                            multiply(lent, step + 1)
-                        elif lent != pairs[-1][1]:
-                            finish(lent, nc.gpsimd)
-                        waiting = (own, step)
-                renew(waiting[0], waiting[1])
-                finish(pairs[0][0], nc.vector)
-                finish(pairs[-1][1], nc.vector)
-                finish(pairs[-1][0], nc.vector)
+                for n in range(turns + BATCH_TILES):
+                    if BATCH_TILES <= n < turns:
+                        multiply(n % BATCH_TILES, n // BATCH_TILES)
+                    if n >= turns:
+                        finish(n - turns)
+                    if 0 <= n - 1 < turns:
+                        copy_out((n - 1) % BATCH_TILES)
+                    if 0 <= n - 2 < turns:
+                        renew((n - 2) % BATCH_TILES, (n - 2) // BATCH_TILES)
+                    if n < turns:
+                        add_blocks(n % BATCH_TILES, n // BATCH_TILES, range(0, HI // 2))
+                    if 0 <= n - 1 < turns:
+                        flip_sums((n - 1) % BATCH_TILES)
+                    if n < turns:
+                        add_blocks(n % BATCH_TILES, n // BATCH_TILES, range(HI // 2, HI))

@@ -26,13 +26,17 @@ BANKS = 8
 W_CHUNK = 1024
 CHUNK_TILES = W_CHUNK // P
 AHEAD = 3
+GROUPED_BUFS = 3
+ACTS_BUFS = 2
 RUN = 4
 VECTOR_COLS = 448
-LO = P // SIDE
-HI = SIDE // LO
+I_LO = P // SIDE
 D_TILES = DOUT // P
 HALVES = DOUT // BANK
+PER_HALF = BANK // P
 LINEAR_FROM = 30.0
+OWN_TILES = 2
+VECTOR_SUMS = 24
 TINY = 1e-24
 
 FLOPS = 2 * BATCH * HID * (HID + DOUT)
@@ -51,31 +55,24 @@ def tile_matchingnet_pa_kernel(tc, h3, W4, b4, W5, b5, out):
 
         ident = consts.tile([P, P], F32, name="ident")
         make_identity(nc, ident[:])
-        orders = {}
-        for label in ("col", "row"):
-            orders[label] = consts.tile([P, P], F32, name="order_" + label)
+        swap = consts.tile([P, P], F32, name="swap")
         nc.vector.tensor_copy(
-            out=orders["col"][:].rearrange("p (j i) -> p j i", i=LO),
-            in_=ident[:].rearrange("p (i j) -> p j i", i=LO),
-        )
-        nc.vector.tensor_copy(
-            out=orders["row"][:].rearrange("p (a i l) -> p a i l", i=LO, l=LO),
-            in_=ident[:].rearrange("p (i a l) -> p a i l", i=LO, l=LO),
+            out=swap[:].rearrange("p (j i) -> p j i", i=I_LO),
+            in_=ident[:].rearrange("p (i j) -> p j i", i=I_LO),
         )
 
-        z_banks = []
         with ExitStack() as front:
             keep = front.enter_context(tc.tile_pool(name="keep", bufs=1))
             wraw = front.enter_context(tc.tile_pool(name="wraw", bufs=AHEAD + 1))
-            stage = front.enter_context(tc.tile_pool(name="stage", bufs=3))
-            acts = front.enter_context(tc.tile_pool(name="acts", bufs=2))
+            stage = front.enter_context(tc.tile_pool(name="stage", bufs=GROUPED_BUFS))
+            acts = front.enter_context(tc.tile_pool(name="acts", bufs=ACTS_BUFS))
 
             chunks = [("w4", block, g) for block in range(HID // W_CHUNK) for g in range(PASSES)]
             chunks += [("w5", 0, g) for g in range(PASSES)]
             raws = {}
 
-            def load(c):
-                weights, block, g = chunks[c]
+            def load(n):
+                weights, block, g = chunks[n]
                 raw = wraw.tile([P, PACK, W_CHUNK], BF16, name="raw")
                 cols = slice(W_CHUNK * block, W_CHUNK * (block + 1))
                 if weights == "w4":
@@ -83,20 +80,20 @@ def tile_matchingnet_pa_kernel(tc, h3, W4, b4, W5, b5, out):
                         first = K_PASS * g + (K_PASS // 2) * u
                         rows = W4[first : first + K_PASS // 2, cols]
                         nc.sync.dma_start(
-                            out=raw[:, 2 * u : 2 * u + 2, :], in_=rows.rearrange("(q e) c -> q e c", e=2)
+                            out=raw[:, 2 * u : 2 * u + 2, :], in_=rows.rearrange("(q e) w -> q e w", e=2)
                         )
                 else:
                     rows = W5[K_PASS * g : K_PASS * (g + 1), cols]
-                    nc.sync.dma_start(out=raw[:], in_=rows.rearrange("(t p) n -> p t n", p=P))
-                raws[c] = raw
+                    nc.sync.dma_start(out=raw[:], in_=rows.rearrange("(t p) w -> p t w", p=P))
+                raws[n] = raw
 
             h3_rows = [keep.tile([P, HID], BF16, name="h3_rows%d" % bt) for bt in range(BATCH_TILES)]
             for bt in range(BATCH_TILES):
                 nc.sync.dma_start(out=h3_rows[bt][:], in_=h3[bt * P : (bt + 1) * P, :])
                 if bt == BATCH_TILES // 2 - 1:
                     load(0)
-            for c in range(1, AHEAD):
-                load(c)
+            for n in range(1, AHEAD):
+                load(n)
 
             h3_grouped = [
                 keep.tile([P, BATCH * PACK], BF16, align_bytes=64, name="h3_grouped%d" % g) for g in range(PASSES)
@@ -106,18 +103,18 @@ def tile_matchingnet_pa_kernel(tc, h3, W4, b4, W5, b5, out):
             for pair in range(BATCH_TILES // 2):
                 for g in range(PASSES):
                     flipped = banks.tile([P, 2, 2, P], F32, tag="bank", name="flipped")
-                    for c in range(2):
-                        words = h3_rows[2 * pair + c][:].bitcast(F32)
+                    for member in range(2):
+                        words = h3_rows[2 * pair + member][:].bitcast(F32)
                         for u in range(2):
                             first = (K_PASS // 2) * g + P * u
-                            nc.tensor.transpose(flipped[:, c, u, :], words[:, first : first + P], ident[:])
+                            nc.tensor.transpose(flipped[:, member, u, :], words[:, first : first + P], ident[:])
                     dst = (
                         h3_grouped[g][:]
                         .bitcast(F32)
                         .rearrange("p (b u) -> p b u", u=2)[:, 2 * P * pair : 2 * P * (pair + 1), :]
-                        .rearrange("p (c b) u -> p c b u", c=2)
+                        .rearrange("p (y b) u -> p y b u", y=2)
                     )
-                    src = flipped[:].rearrange("p c u b -> p c b u")
+                    src = flipped[:].rearrange("p y u b -> p y b u")
                     if g % 2 == 0:
                         nc.vector.tensor_copy(out=dst, in_=src)
                     else:
@@ -130,8 +127,8 @@ def tile_matchingnet_pa_kernel(tc, h3, W4, b4, W5, b5, out):
             b4_rows = HID // P
             bias_rows = consts.tile([P, P], BF16, name="bias_rows")
             nc.vector.memset(bias_rows[:], 0.0)
-            nc.sync.dma_start(out=bias_rows[0:b4_rows, :], in_=b4.rearrange("(r c) -> r c", c=P))
-            nc.sync.dma_start(out=bias_rows[b4_rows : b4_rows + D_TILES, :], in_=b5.rearrange("(r c) -> r c", c=P))
+            nc.sync.dma_start(out=bias_rows[0:b4_rows, :], in_=b4.rearrange("(row col) -> row col", col=P))
+            nc.sync.dma_start(out=bias_rows[b4_rows : b4_rows + D_TILES, :], in_=b5.rearrange("(row col) -> row col", col=P))
             bias_rows_f32 = consts.tile([P, P], F32, name="bias_rows_f32")
             nc.vector.tensor_copy(out=bias_rows_f32[:], in_=bias_rows[:])
             bias_bank = banks.tile([P, P], F32, tag="bank", name="bias_bank")
@@ -150,25 +147,24 @@ def tile_matchingnet_pa_kernel(tc, h3, W4, b4, W5, b5, out):
             h4_codes = keep.tile([P, PASSES, BATCH], U32, align_bytes=64, name="h4_codes")
             h4_scales = keep.tile([P, PASSES, BATCH], U8, align_bytes=64, name="h4_scales")
             moving = {"w4": (h3_codes, h3_scales), "w5": (h4_codes, h4_scales)}
-
             groupeds = {}
 
-            def regroup(c):
+            def regroup(n):
                 grouped = stage.tile([P, W_CHUNK, PACK], BF16, align_bytes=64, name="grouped")
-                src = raws[c][:].rearrange("p t (c i) -> p c t i", i=RUN)
-                dst = grouped[:].rearrange("p (c i) t -> p c t i", i=RUN)
+                src = raws[n][:].rearrange("p t (w r) -> p w t r", r=RUN)
+                dst = grouped[:].rearrange("p (w r) t -> p w t r", r=RUN)
                 cut = VECTOR_COLS // RUN
                 nc.vector.tensor_copy(out=dst[:, :cut], in_=src[:, :cut])
                 nc.scalar.copy(out=dst[:, cut:], in_=src[:, cut:])
-                groupeds[c] = grouped
+                groupeds[n] = grouped
 
-            def quantise_and_multiply(c, sums_banks):
-                weights, block, g = chunks[c]
+            def quantise_and_multiply(n, sums_banks):
+                weights, block, g = chunks[n]
                 cols = slice(W_CHUNK * block, W_CHUNK * (block + 1))
                 nc.vector.quantize_mx(
                     out=w_codes[weights][:, g, cols].bitcast(FP8X4),
                     scales=w_scales[weights][:, g, cols],
-                    in_=groupeds[c][:].rearrange("p w t -> p (w t)"),
+                    in_=groupeds[n][:].rearrange("p w t -> p (w t)"),
                 )
                 for m in range(CHUNK_TILES):
                     first = W_CHUNK * block + P * m
@@ -207,18 +203,18 @@ def tile_matchingnet_pa_kernel(tc, h3, W4, b4, W5, b5, out):
                     )
 
             sums_banks = []
-            for c in range(len(chunks) + 1):
-                if c + AHEAD < len(chunks):
-                    load(c + AHEAD)
-                if c < len(chunks):
-                    regroup(c)
-                if c > 0:
-                    weights, block, g = chunks[c - 1]
+            for n in range(len(chunks) + 1):
+                if n + AHEAD < len(chunks):
+                    load(n + AHEAD)
+                if n < len(chunks):
+                    regroup(n)
+                if n > 0:
+                    weights, block, g = chunks[n - 1]
                     if g == 0:
                         sums_banks = [
                             banks.tile([P, BANK], F32, tag="bank", name="sums_bank%d" % m) for m in range(CHUNK_TILES)
                         ]
-                    quantise_and_multiply(c - 1, sums_banks)
+                    quantise_and_multiply(n - 1, sums_banks)
                     if weights == "w4" and g == PASSES - 1:
                         activate(block, sums_banks)
             z_banks = sums_banks
@@ -235,41 +231,45 @@ def tile_matchingnet_pa_kernel(tc, h3, W4, b4, W5, b5, out):
                 )
                 nc.scalar.activation(out=expo[:, d, :], in_=expo[:, d, :], func=ACT.Exp)
 
-            matrices = {}
-            for label in ("col", "row"):
-                matrices[label] = [soft.tile([P, DOUT], F32, name="r_%s_%d" % (label, bt)) for bt in range(BATCH_TILES)]
-            per_half = BANK // P
+            own_tiles = range(OWN_TILES)
+            lent_tiles = range(OWN_TILES, BATCH_TILES)
+            orders = {"col": swap, "row": ident}
+            matrices = {"col": {}, "row": {}}
 
-            def flip_back(label, bt, h, engine_copy):
+            def flip_back(label, bt, h):
                 bank = banks.tile([P, BANK], F32, tag="bank", name="r_bank")
-                for q in range(per_half):
+                for part in range(PER_HALF):
                     nc.tensor.transpose(
-                        bank[:, P * q : P * (q + 1)],
-                        r_flipped[:, per_half * h + q, P * bt : P * (bt + 1)],
+                        bank[:, P * part : P * (part + 1)],
+                        r_flipped[:, PER_HALF * h + part, P * bt : P * (bt + 1)],
                         orders[label][:],
                     )
-                if label == "col":
-                    engine_copy(out=matrices[label][bt][:, BANK * h : BANK * (h + 1)], in_=bank[:])
-                else:
-                    engine_copy(
-                        out=matrices[label][bt][:].rearrange("p (a d x) -> p d a x", a=HI, d=HI)[
-                            :, per_half * h : per_half * (h + 1)
-                        ],
-                        in_=bank[:].rearrange("p (d a x) -> p d a x", d=per_half, a=HI),
-                    )
+                return bank
 
+            for label in ("col", "row"):
+                for bt in lent_tiles:
+                    matrices[label][bt] = [soft.tile([P, DOUT], F32, name="r_%s_%d" % (label, bt))]
+            staged = []
             for h in range(HALVES):
-                for q in range(per_half):
-                    d = per_half * h + q
+                for part in range(PER_HALF):
+                    d = PER_HALF * h + part
                     b5_col = bias_cols[:, b4_rows + d : b4_rows + d + 1]
                     nc.scalar.activation(out=expo[:, d, :], in_=expo[:, d, :], func=ACT.Ln, bias=1.0, scale=1.0)
                     nc.vector.scalar_tensor_tensor(
                         out=r_flipped[:, d, :], in0=z_banks[d][:], scalar=b5_col, in1=expo[:, d, :], op0=ALU.add, op1=ALU.max
                     )
-            for label in ("col", "row"):
-                for bt in range(BATCH_TILES):
-                    flip_back(label, bt, 0, nc.vector.tensor_copy)
-                    flip_back(label, bt, 1, nc.scalar.copy)
+                for label in ("col", "row"):
+                    for bt in lent_tiles:
+                        staged.append((label, bt, h, flip_back(label, bt, h)))
+            for label, bt, h, bank in staged:
+                in_sbuf = matrices[label][bt][0][:, BANK * h : BANK * (h + 1)]
+                if label == "col":
+                    nc.vector.tensor_copy(out=in_sbuf, in_=bank[:])
+                else:
+                    nc.scalar.copy(out=in_sbuf, in_=bank[:])
+            for bt in own_tiles:
+                for label in ("col", "row"):
+                    matrices[label][bt] = [flip_back(label, bt, h) for h in range(HALVES)]
             nc.scalar.activation(out=warm[:], in_=tiny[:], func=ACT.Abs_reciprocal_sqrt)
 
             state = []
@@ -277,105 +277,113 @@ def tile_matchingnet_pa_kernel(tc, h3, W4, b4, W5, b5, out):
                 vectors = {}
                 for name in ("a", "c"):
                     vectors[name] = soft.tile([P, SIDE], F32, name="%s%d" % (name, bt))
-                    vectors["floor_" + name] = soft.tile([P, SIDE], F32, name="floor_%s%d" % (name, bt))
-                    nc.vector.memset(vectors["floor_" + name][:], 1.0)
-                vectors["sums"] = soft.tile([P, SIDE], F32, name="sums%d" % bt)
+                    vectors["bounds_" + name] = soft.tile([P, 2, SIDE], F32, name="bounds_%s%d" % (name, bt))
+                    nc.vector.memset(vectors["bounds_" + name][:, 1, :], EPS)
+                vectors["divisor"] = soft.tile([P, SIDE], F32, name="divisor%d" % bt)
                 vectors["root"] = soft.tile([P, SIDE], F32, name="root%d" % bt)
                 vectors["prod"] = soft.tile([P, DOUT], F32, name="prod%d" % bt)
-                vectors["partial"] = soft.tile([P, P], F32, name="partial%d" % bt)
                 state.append(vectors)
+            for bt in own_tiles:
+                nc.vector.memset(state[bt]["a"][:], 1.0)
+            unused = {bt: soft.tile([P, SIDE - VECTOR_SUMS, SIDE], F32, name="unused%d" % bt) for bt in lent_tiles}
 
-            def label_of(step):
-                return "col" if step % 2 == 0 else "row"
-
-            def old_factor(step):
-                return "a" if step % 2 == 0 else "c"
-
-            def new_factor(step):
+            def factor_of(step):
                 return "c" if step % 2 == 0 else "a"
 
-            def spread(vector):
-                return vector[:].rearrange("p (d l) -> p d l", l=LO).unsqueeze(2).to_broadcast([P, HI, SIDE, LO])
+            def multiply(bt, step):
+                engine = nc.vector if bt in own_tiles else nc.gpsimd
+                vectors = state[bt]
+                pieces = matrices["col" if step % 2 == 0 else "row"][bt]
+                width = DOUT // len(pieces)
+                span = width // SIDE
+                for h, piece in enumerate(pieces):
+                    target = vectors["prod"][:, width * h : width * (h + 1)]
+                    if step % 2 == 0:
+                        a_here = vectors["a"][:, span * h : span * (h + 1)].rearrange("p (d i) -> p d i", i=I_LO)
+                        engine.tensor_tensor(
+                            out=target.rearrange("p (d j i) -> p d j i", j=SIDE, i=I_LO),
+                            in0=piece[:].rearrange("p (d j i) -> p d j i", j=SIDE, i=I_LO),
+                            in1=a_here.unsqueeze(2).to_broadcast([P, span // I_LO, SIDE, I_LO]),
+                            op=ALU.mult,
+                        )
+                    else:
+                        engine.tensor_tensor(
+                            out=target.rearrange("p (i j) -> p i j", j=SIDE),
+                            in0=piece[:].rearrange("p (i j) -> p i j", j=SIDE),
+                            in1=vectors["c"][:].unsqueeze(1).to_broadcast([P, span, SIDE]),
+                            op=ALU.mult,
+                        )
 
             def terms_of(bt, step):
-                return matrices["col"][bt] if step == 0 else state[bt]["prod"]
+                if step == 0 and bt in lent_tiles:
+                    terms = matrices["col"][bt][0][:]
+                else:
+                    terms = state[bt]["prod"][:]
+                if step % 2 == 0:
+                    return terms.rearrange("p (d j i) -> p j d i", j=SIDE, i=I_LO)
+                return terms.rearrange("p (i j) -> p i j", j=SIDE)
 
-            def multiply(bt, step):
-                for blocks in (slice(0, HI // 2), slice(HI // 2, HI)):
-                    nc.vector.tensor_tensor(
-                        out=state[bt]["prod"][:].rearrange("p (d m l) -> p d m l", m=SIDE, l=LO)[:, blocks],
-                        in0=matrices[label_of(step)][bt][:].rearrange("p (d m l) -> p d m l", m=SIDE, l=LO)[:, blocks],
-                        in1=spread(state[bt][old_factor(step)])[:, blocks],
-                        op=ALU.mult,
-                    )
+            def add_up_on_vector(bt, step, count):
+                sums = state[bt]["bounds_" + factor_of(step)][:, 0, :]
+                nc.vector.tensor_reduce(
+                    out=sums[:, :count],
+                    in_=terms_of(bt, step)[:, :count],
+                    axis=AXIS.XY if step % 2 == 0 else AXIS.X,
+                    op=ALU.add,
+                )
 
-            folded_banks = {}
-            upright_banks = {}
-
-            def add_blocks(bt, step, blocks):
-                if blocks[0] == 0:
-                    folded_banks[bt] = banks.tile([P, P], F32, tag="bank", name="folded")
-                for d in blocks:
-                    nc.tensor.matmul(
-                        out=folded_banks[bt][:],
-                        lhsT=terms_of(bt, step)[:, P * d : P * (d + 1)],
-                        rhs=ident[:],
-                        start=(d == 0),
-                        stop=(d == HI - 1),
-                        is_transpose=True,
-                    )
-
-            def copy_out(bt):
-                nc.scalar.copy(out=state[bt]["partial"][:], in_=folded_banks[bt][:])
-
-            def flip_sums(bt):
-                upright = banks.tile([P, P], F32, tag="bank", name="upright")
-                nc.tensor.transpose(upright[:], state[bt]["partial"][:], ident[:])
-                upright_banks[bt] = upright
+            def add_up_on_scalar(bt, step, done):
+                sums = state[bt]["bounds_" + factor_of(step)][:, 0, :]
+                terms = terms_of(bt, step)
+                for s in range(done, SIDE):
+                    copied = unused[bt][:, s - done, :]
+                    if step % 2 == 0:
+                        copied = copied.rearrange("p (d i) -> p d i", i=I_LO)
+                    nc.scalar.activation(out=copied, in_=terms[:, s], func=ACT.Copy, accum_out=sums[:, s : s + 1])
 
             def renew(bt, step):
                 vectors = state[bt]
-                factor = new_factor(step)
-                floor = vectors["floor_" + factor]
+                factor = factor_of(step)
+                bounds = vectors["bounds_" + factor]
                 nc.vector.tensor_reduce(
-                    out=vectors["sums"][:],
-                    in_=upright_banks[bt][:].rearrange("p (m l) -> p m l", l=LO),
-                    axis=AXIS.X,
-                    op=ALU.add,
-                )
-                nc.vector.scalar_tensor_tensor(
-                    out=floor[:], in0=floor[:], scalar=EPS, in1=vectors["sums"][:], op0=ALU.mult, op1=ALU.max
+                    out=vectors["divisor"][:], in_=bounds[:].rearrange("p plane s -> p s plane"), axis=AXIS.X, op=ALU.max
                 )
                 nc.scalar.activation(
-                    out=vectors["root"][:], in_=floor[:], func=ACT.Abs_reciprocal_sqrt, bias=tiny[:], scale=1.0
+                    out=vectors["root"][:], in_=vectors["divisor"][:], func=ACT.Abs_reciprocal_sqrt, bias=tiny[:], scale=1.0
                 )
                 nc.scalar.activation(out=vectors[factor][:], in_=vectors["root"][:], func=ACT.Square)
+                nc.scalar.mul(out=bounds[:, 1, :], in_=vectors["divisor"][:], mul=EPS)
 
-            def finish(bt):
+            def finish(bt, engine):
                 vectors = state[bt]
-                result = soft.tile([P, DOUT], F32, name="result%d" % bt)
-                nc.vector.tensor_tensor(
-                    out=result[:].rearrange("p (i a l) -> p i a l", a=HI, l=LO),
-                    in0=vectors["prod"][:].rearrange("p (a i l) -> p i a l", a=HI, l=LO),
-                    in1=vectors["a"][:].unsqueeze(2).unsqueeze(3).to_broadcast([P, SIDE, HI, LO]),
+                by_matrix = vectors["prod"][:].rearrange("p (i j) -> p i j", j=SIDE)
+                engine.tensor_tensor(
+                    out=by_matrix,
+                    in0=by_matrix,
+                    in1=vectors["a"][:].unsqueeze(2).to_broadcast([P, SIDE, SIDE]),
                     op=ALU.mult,
                 )
-                nc.sync.dma_start(out=out[P * bt : P * (bt + 1)].rearrange("b i j -> b (i j)"), in_=result[:])
+                nc.sync.dma_start(out=out[P * bt : P * (bt + 1)].rearrange("b i j -> b (i j)"), in_=vectors["prod"][:])
 
-            turns = 2 * ROUNDS * BATCH_TILES
+            steps = 2 * ROUNDS
+            pairs = [(bt, bt + OWN_TILES) for bt in own_tiles]
             with tc.manual_schedule():
-                for n in range(turns + BATCH_TILES):
-                    if BATCH_TILES <= n < turns:
-                        multiply(n % BATCH_TILES, n // BATCH_TILES)
-                    if n >= turns:
-                        finish(n - turns)
-                    if 0 <= n - 1 < turns:
-                        copy_out((n - 1) % BATCH_TILES)
-                    if 0 <= n - 2 < turns:
-                        renew((n - 2) % BATCH_TILES, (n - 2) // BATCH_TILES)
-                    if n < turns:
-                        add_blocks(n % BATCH_TILES, n // BATCH_TILES, range(0, HI // 2))
-                    if 0 <= n - 1 < turns:
-                        flip_sums((n - 1) % BATCH_TILES)
-                    if n < turns:
-                        add_blocks(n % BATCH_TILES, n // BATCH_TILES, range(HI // 2, HI))
+                waiting = None
+                for step in range(steps):
+                    for own, lent in pairs:
+                        add_up_on_scalar(lent, step, VECTOR_SUMS)
+                        multiply(own, step)
+                        if waiting is not None:
+                            renew(waiting[0], waiting[1])
+                        add_up_on_vector(lent, step, VECTOR_SUMS)
+                        add_up_on_vector(own, step, SIDE)
+                        renew(lent, step)
+                        if step + 1 < steps:
+                            multiply(lent, step + 1)
+                        elif lent != pairs[-1][1]:
+                            finish(lent, nc.gpsimd)
+                        waiting = (own, step)
+                renew(waiting[0], waiting[1])
+                finish(pairs[0][0], nc.vector)
+                finish(pairs[-1][1], nc.vector)
+                finish(pairs[-1][0], nc.vector)

from contextlib import ExitStack

import concourse.mybir as mybir
from concourse.masks import make_identity

F32 = mybir.dt.float32
BF16 = mybir.dt.bfloat16
U32 = mybir.dt.uint32
U8 = mybir.dt.uint8
FP8X4 = mybir.dt.float8_e4m3fn_x4
ALU = mybir.AluOpType
ACT = mybir.ActivationFunctionType
AXIS = mybir.AxisListType

P = 128
PACK = 4
K_PASS = P * PACK
BATCH, SIDE, HID, ROUNDS = 512, 32, 2048, 10
DOUT = SIDE * SIDE
SLOPE = 0.01
EPS = 1e-8
PASSES = HID // K_PASS
BATCH_TILES = BATCH // P
BANK = 512
BANKS = 8
W_CHUNK = 1024
CHUNK_TILES = W_CHUNK // P
AHEAD = 3
GROUPED_BUFS = 3
ACTS_BUFS = 2
RUN = 4
VECTOR_COLS = 448
I_LO = P // SIDE
D_TILES = DOUT // P
HALVES = DOUT // BANK
PER_HALF = BANK // P
LINEAR_FROM = 30.0
OWN_TILES = 2
VECTOR_SUMS = 24
TINY = 1e-24

FLOPS = 2 * BATCH * HID * (HID + DOUT)


def tile_matchingnet_pa_kernel(tc, h3, W4, b4, W5, b5, out):
    nc = tc.nc
    with ExitStack() as whole:
        consts = whole.enter_context(tc.tile_pool(name="consts", bufs=1))
        banks = whole.enter_context(tc.psum_pool(name="banks", bufs=BANKS))

        tiny = consts.tile([P, 1], F32, name="tiny")
        nc.vector.memset(tiny[:], TINY)
        warm = consts.tile([P, 1], F32, name="warm")
        nc.scalar.activation(out=warm[:], in_=tiny[:], func=ACT.Exp)

        ident = consts.tile([P, P], F32, name="ident")
        make_identity(nc, ident[:])
        swap = consts.tile([P, P], F32, name="swap")
        nc.vector.tensor_copy(
            out=swap[:].rearrange("p (j i) -> p j i", i=I_LO),
            in_=ident[:].rearrange("p (i j) -> p j i", i=I_LO),
        )

        with ExitStack() as front:
            keep = front.enter_context(tc.tile_pool(name="keep", bufs=1))
            wraw = front.enter_context(tc.tile_pool(name="wraw", bufs=AHEAD + 1))
            stage = front.enter_context(tc.tile_pool(name="stage", bufs=GROUPED_BUFS))
            acts = front.enter_context(tc.tile_pool(name="acts", bufs=ACTS_BUFS))

            chunks = [("w4", block, g) for block in range(HID // W_CHUNK) for g in range(PASSES)]
            chunks += [("w5", 0, g) for g in range(PASSES)]
            raws = {}

            def load(n):
                weights, block, g = chunks[n]
                raw = wraw.tile([P, PACK, W_CHUNK], BF16, name="raw")
                cols = slice(W_CHUNK * block, W_CHUNK * (block + 1))
                if weights == "w4":
                    for u in range(2):
                        first = K_PASS * g + (K_PASS // 2) * u
                        rows = W4[first : first + K_PASS // 2, cols]
                        nc.sync.dma_start(
                            out=raw[:, 2 * u : 2 * u + 2, :], in_=rows.rearrange("(q e) w -> q e w", e=2)
                        )
                else:
                    rows = W5[K_PASS * g : K_PASS * (g + 1), cols]
                    nc.sync.dma_start(out=raw[:], in_=rows.rearrange("(t p) w -> p t w", p=P))
                raws[n] = raw

            h3_rows = [keep.tile([P, HID], BF16, name="h3_rows%d" % bt) for bt in range(BATCH_TILES)]
            for bt in range(BATCH_TILES):
                nc.sync.dma_start(out=h3_rows[bt][:], in_=h3[bt * P : (bt + 1) * P, :])
                if bt == BATCH_TILES // 2 - 1:
                    load(0)
            for n in range(1, AHEAD):
                load(n)

            h3_grouped = [
                keep.tile([P, BATCH * PACK], BF16, align_bytes=64, name="h3_grouped%d" % g) for g in range(PASSES)
            ]
            h3_codes = keep.tile([P, PASSES, BATCH], U32, align_bytes=64, name="h3_codes")
            h3_scales = keep.tile([P, PASSES, BATCH], U8, align_bytes=64, name="h3_scales")
            for pair in range(BATCH_TILES // 2):
                for g in range(PASSES):
                    flipped = banks.tile([P, 2, 2, P], F32, tag="bank", name="flipped")
                    for member in range(2):
                        words = h3_rows[2 * pair + member][:].bitcast(F32)
                        for u in range(2):
                            first = (K_PASS // 2) * g + P * u
                            nc.tensor.transpose(flipped[:, member, u, :], words[:, first : first + P], ident[:])
                    dst = (
                        h3_grouped[g][:]
                        .bitcast(F32)
                        .rearrange("p (b u) -> p b u", u=2)[:, 2 * P * pair : 2 * P * (pair + 1), :]
                        .rearrange("p (y b) u -> p y b u", y=2)
                    )
                    src = flipped[:].rearrange("p y u b -> p y b u")
                    if g % 2 == 0:
                        nc.vector.tensor_copy(out=dst, in_=src)
                    else:
                        nc.scalar.copy(out=dst, in_=src)
            for g in range(PASSES):
                nc.vector.quantize_mx(
                    out=h3_codes[:, g, :].bitcast(FP8X4), scales=h3_scales[:, g, :], in_=h3_grouped[g][:]
                )

            b4_rows = HID // P
            bias_rows = consts.tile([P, P], BF16, name="bias_rows")
            nc.vector.memset(bias_rows[:], 0.0)
            nc.sync.dma_start(out=bias_rows[0:b4_rows, :], in_=b4.rearrange("(row col) -> row col", col=P))
            nc.sync.dma_start(out=bias_rows[b4_rows : b4_rows + D_TILES, :], in_=b5.rearrange("(row col) -> row col", col=P))
            bias_rows_f32 = consts.tile([P, P], F32, name="bias_rows_f32")
            nc.vector.tensor_copy(out=bias_rows_f32[:], in_=bias_rows[:])
            bias_bank = banks.tile([P, P], F32, tag="bank", name="bias_bank")
            nc.tensor.transpose(bias_bank[:], bias_rows_f32[:], ident[:])
            bias_cols = consts.tile([P, b4_rows + D_TILES], F32, name="bias_cols")
            nc.vector.tensor_copy(out=bias_cols[:], in_=bias_bank[:, 0 : b4_rows + D_TILES])

            w_codes = {
                "w4": keep.tile([P, PASSES, HID], U32, align_bytes=64, name="w4_codes"),
                "w5": keep.tile([P, PASSES, DOUT], U32, align_bytes=64, name="w5_codes"),
            }
            w_scales = {
                "w4": keep.tile([P, PASSES, HID], U8, align_bytes=64, name="w4_scales"),
                "w5": keep.tile([P, PASSES, DOUT], U8, align_bytes=64, name="w5_scales"),
            }
            h4_codes = keep.tile([P, PASSES, BATCH], U32, align_bytes=64, name="h4_codes")
            h4_scales = keep.tile([P, PASSES, BATCH], U8, align_bytes=64, name="h4_scales")
            moving = {"w4": (h3_codes, h3_scales), "w5": (h4_codes, h4_scales)}
            groupeds = {}

            def regroup(n):
                grouped = stage.tile([P, W_CHUNK, PACK], BF16, align_bytes=64, name="grouped")
                src = raws[n][:].rearrange("p t (w r) -> p w t r", r=RUN)
                dst = grouped[:].rearrange("p (w r) t -> p w t r", r=RUN)
                cut = VECTOR_COLS // RUN
                nc.vector.tensor_copy(out=dst[:, :cut], in_=src[:, :cut])
                nc.scalar.copy(out=dst[:, cut:], in_=src[:, cut:])
                groupeds[n] = grouped

            def quantise_and_multiply(n, sums_banks):
                weights, block, g = chunks[n]
                cols = slice(W_CHUNK * block, W_CHUNK * (block + 1))
                nc.vector.quantize_mx(
                    out=w_codes[weights][:, g, cols].bitcast(FP8X4),
                    scales=w_scales[weights][:, g, cols],
                    in_=groupeds[n][:].rearrange("p w t -> p (w t)"),
                )
                for m in range(CHUNK_TILES):
                    first = W_CHUNK * block + P * m
                    nc.tensor.matmul_mx(
                        out=sums_banks[m][:],
                        lhsT=w_codes[weights][:, g, first : first + P].bitcast(FP8X4),
                        lhsT_scale=w_scales[weights][:, g, first : first + P],
                        rhs=moving[weights][0][:, g, :].bitcast(FP8X4),
                        rhs_scale=moving[weights][1][:, g, :],
                        start=(g == 0),
                        stop=(g == PASSES - 1),
                    )

            def activate(block, sums_banks):
                for quad in range(CHUNK_TILES // PACK):
                    g2 = (CHUNK_TILES // PACK) * block + quad
                    biased = acts.tile([P, PACK, BATCH], F32, name="biased")
                    for t in range(PACK):
                        m = PACK * g2 + t
                        nc.scalar.activation(
                            out=biased[:, t, :],
                            in_=sums_banks[PACK * quad + t][:],
                            func=ACT.Identity,
                            bias=bias_cols[:, m : m + 1],
                            scale=1.0,
                        )
                    h4_grouped = acts.tile([P, BATCH, PACK], BF16, align_bytes=64, name="h4_grouped")
                    by_column = biased[:].rearrange("p t b -> p b t")
                    nc.vector.scalar_tensor_tensor(
                        out=h4_grouped[:], in0=by_column, scalar=SLOPE, in1=by_column, op0=ALU.mult, op1=ALU.max
                    )
                    nc.vector.quantize_mx(
                        out=h4_codes[:, g2, :].bitcast(FP8X4),
                        scales=h4_scales[:, g2, :],
                        in_=h4_grouped[:].rearrange("p b t -> p (b t)"),
                    )

            sums_banks = []
            for n in range(len(chunks) + 1):
                if n + AHEAD < len(chunks):
                    load(n + AHEAD)
                if n < len(chunks):
                    regroup(n)
                if n > 0:
                    weights, block, g = chunks[n - 1]
                    if g == 0:
                        sums_banks = [
                            banks.tile([P, BANK], F32, tag="bank", name="sums_bank%d" % m) for m in range(CHUNK_TILES)
                        ]
                    quantise_and_multiply(n - 1, sums_banks)
                    if weights == "w4" and g == PASSES - 1:
                        activate(block, sums_banks)
            z_banks = sums_banks

        with ExitStack() as back:
            soft = back.enter_context(tc.tile_pool(name="soft", bufs=1))

            expo = soft.tile([P, D_TILES, BATCH], F32, name="expo")
            r_flipped = soft.tile([P, D_TILES, BATCH], F32, name="r_flipped")
            for d in range(D_TILES):
                b5_col = bias_cols[:, b4_rows + d : b4_rows + d + 1]
                nc.vector.tensor_scalar(
                    out=expo[:, d, :], in0=z_banks[d][:], scalar1=b5_col, scalar2=LINEAR_FROM, op0=ALU.add, op1=ALU.min
                )
                nc.scalar.activation(out=expo[:, d, :], in_=expo[:, d, :], func=ACT.Exp)

            own_tiles = range(OWN_TILES)
            lent_tiles = range(OWN_TILES, BATCH_TILES)
            orders = {"col": swap, "row": ident}
            matrices = {"col": {}, "row": {}}

            def flip_back(label, bt, h):
                bank = banks.tile([P, BANK], F32, tag="bank", name="r_bank")
                for part in range(PER_HALF):
                    nc.tensor.transpose(
                        bank[:, P * part : P * (part + 1)],
                        r_flipped[:, PER_HALF * h + part, P * bt : P * (bt + 1)],
                        orders[label][:],
                    )
                return bank

            for label in ("col", "row"):
                for bt in lent_tiles:
                    matrices[label][bt] = [soft.tile([P, DOUT], F32, name="r_%s_%d" % (label, bt))]
            staged = []
            for h in range(HALVES):
                for part in range(PER_HALF):
                    d = PER_HALF * h + part
                    b5_col = bias_cols[:, b4_rows + d : b4_rows + d + 1]
                    nc.scalar.activation(out=expo[:, d, :], in_=expo[:, d, :], func=ACT.Ln, bias=1.0, scale=1.0)
                    nc.vector.scalar_tensor_tensor(
                        out=r_flipped[:, d, :], in0=z_banks[d][:], scalar=b5_col, in1=expo[:, d, :], op0=ALU.add, op1=ALU.max
                    )
                for label in ("col", "row"):
                    for bt in lent_tiles:
                        staged.append((label, bt, h, flip_back(label, bt, h)))
            for label, bt, h, bank in staged:
                in_sbuf = matrices[label][bt][0][:, BANK * h : BANK * (h + 1)]
                if label == "col":
                    nc.vector.tensor_copy(out=in_sbuf, in_=bank[:])
                else:
                    nc.scalar.copy(out=in_sbuf, in_=bank[:])
            for bt in own_tiles:
                for label in ("col", "row"):
                    matrices[label][bt] = [flip_back(label, bt, h) for h in range(HALVES)]
            nc.scalar.activation(out=warm[:], in_=tiny[:], func=ACT.Abs_reciprocal_sqrt)

            state = []
            for bt in range(BATCH_TILES):
                vectors = {}
                for name in ("a", "c"):
                    vectors[name] = soft.tile([P, SIDE], F32, name="%s%d" % (name, bt))
                    vectors["bounds_" + name] = soft.tile([P, 2, SIDE], F32, name="bounds_%s%d" % (name, bt))
                    nc.vector.memset(vectors["bounds_" + name][:, 1, :], EPS)
                vectors["divisor"] = soft.tile([P, SIDE], F32, name="divisor%d" % bt)
                vectors["root"] = soft.tile([P, SIDE], F32, name="root%d" % bt)
                vectors["prod"] = soft.tile([P, DOUT], F32, name="prod%d" % bt)
                state.append(vectors)
            for bt in own_tiles:
                nc.vector.memset(state[bt]["a"][:], 1.0)
            unused = {bt: soft.tile([P, SIDE - VECTOR_SUMS, SIDE], F32, name="unused%d" % bt) for bt in lent_tiles}

            def factor_of(step):
                return "c" if step % 2 == 0 else "a"

            def multiply(bt, step):
                engine = nc.vector if bt in own_tiles else nc.gpsimd
                vectors = state[bt]
                pieces = matrices["col" if step % 2 == 0 else "row"][bt]
                width = DOUT // len(pieces)
                span = width // SIDE
                for h, piece in enumerate(pieces):
                    target = vectors["prod"][:, width * h : width * (h + 1)]
                    if step % 2 == 0:
                        a_here = vectors["a"][:, span * h : span * (h + 1)].rearrange("p (d i) -> p d i", i=I_LO)
                        engine.tensor_tensor(
                            out=target.rearrange("p (d j i) -> p d j i", j=SIDE, i=I_LO),
                            in0=piece[:].rearrange("p (d j i) -> p d j i", j=SIDE, i=I_LO),
                            in1=a_here.unsqueeze(2).to_broadcast([P, span // I_LO, SIDE, I_LO]),
                            op=ALU.mult,
                        )
                    else:
                        engine.tensor_tensor(
                            out=target.rearrange("p (i j) -> p i j", j=SIDE),
                            in0=piece[:].rearrange("p (i j) -> p i j", j=SIDE),
                            in1=vectors["c"][:].unsqueeze(1).to_broadcast([P, span, SIDE]),
                            op=ALU.mult,
                        )

            def terms_of(bt, step):
                if step == 0 and bt in lent_tiles:
                    terms = matrices["col"][bt][0][:]
                else:
                    terms = state[bt]["prod"][:]
                if step % 2 == 0:
                    return terms.rearrange("p (d j i) -> p j d i", j=SIDE, i=I_LO)
                return terms.rearrange("p (i j) -> p i j", j=SIDE)

            def add_up_on_vector(bt, step, count):
                sums = state[bt]["bounds_" + factor_of(step)][:, 0, :]
                nc.vector.tensor_reduce(
                    out=sums[:, :count],
                    in_=terms_of(bt, step)[:, :count],
                    axis=AXIS.XY if step % 2 == 0 else AXIS.X,
                    op=ALU.add,
                )

            def add_up_on_scalar(bt, step, done):
                sums = state[bt]["bounds_" + factor_of(step)][:, 0, :]
                terms = terms_of(bt, step)
                for s in range(done, SIDE):
                    copied = unused[bt][:, s - done, :]
                    if step % 2 == 0:
                        copied = copied.rearrange("p (d i) -> p d i", i=I_LO)
                    nc.scalar.activation(out=copied, in_=terms[:, s], func=ACT.Copy, accum_out=sums[:, s : s + 1])

            def renew(bt, step):
                vectors = state[bt]
                factor = factor_of(step)
                bounds = vectors["bounds_" + factor]
                nc.vector.tensor_reduce(
                    out=vectors["divisor"][:], in_=bounds[:].rearrange("p plane s -> p s plane"), axis=AXIS.X, op=ALU.max
                )
                nc.scalar.activation(
                    out=vectors["root"][:], in_=vectors["divisor"][:], func=ACT.Abs_reciprocal_sqrt, bias=tiny[:], scale=1.0
                )
                nc.scalar.activation(out=vectors[factor][:], in_=vectors["root"][:], func=ACT.Square)
                nc.scalar.mul(out=bounds[:, 1, :], in_=vectors["divisor"][:], mul=EPS)

            def finish(bt, engine):
                vectors = state[bt]
                by_matrix = vectors["prod"][:].rearrange("p (i j) -> p i j", j=SIDE)
                engine.tensor_tensor(
                    out=by_matrix,
                    in0=by_matrix,
                    in1=vectors["a"][:].unsqueeze(2).to_broadcast([P, SIDE, SIDE]),
                    op=ALU.mult,
                )
                nc.sync.dma_start(out=out[P * bt : P * (bt + 1)].rearrange("b i j -> b (i j)"), in_=vectors["prod"][:])

            steps = 2 * ROUNDS
            pairs = [(bt, bt + OWN_TILES) for bt in own_tiles]
            with tc.manual_schedule():
                waiting = None
                for step in range(steps):
                    for own, lent in pairs:
                        add_up_on_scalar(lent, step, VECTOR_SUMS)
                        multiply(own, step)
                        if waiting is not None:
                            renew(waiting[0], waiting[1])
                        add_up_on_vector(lent, step, VECTOR_SUMS)
                        add_up_on_vector(own, step, SIDE)
                        renew(lent, step)
                        if step + 1 < steps:
                            multiply(lent, step + 1)
                        elif lent != pairs[-1][1]:
                            finish(lent, nc.gpsimd)
                        waiting = (own, step)
                renew(waiting[0], waiting[1])
                finish(pairs[0][0], nc.vector)
                finish(pairs[-1][1], nc.vector)
                finish(pairs[-1][0], nc.vector)
